import numpy as np
import ml_dtypes


def mxq(x, axis, fmt="e4m3"):
    dtype, down = {"e4m3": (ml_dtypes.float8_e4m3fn, 7), "e5m2": (ml_dtypes.float8_e5m2, 14)}[fmt]
    v = np.moveaxis(np.asarray(x, np.float32).astype(ml_dtypes.bfloat16).astype(np.float64), axis, -1)
    blocks = v.reshape(v.shape[:-1] + (-1, 32))
    amax = np.abs(blocks).max(-1, keepdims=True)
    byte = np.maximum(np.where(amax > 0, np.frexp(amax)[1] - 1 + 127, 0) - down, 1)
    scale = np.exp2(byte - 127.0)
    codes = (blocks / scale).astype(np.float32).astype(dtype).astype(np.float64)
    return np.moveaxis((codes * scale).reshape(v.shape), -1, axis)


WIDE = False


def mx_kscale(k):
    if not WIDE:
        return np.ones(k)
    levels = np.array([10, -10, 5, -5, 0])
    a = np.random.permutation(np.resize(levels, k // 512 * 4)).reshape(k // 512, 4)
    idx = np.arange(k)
    return np.exp2(a[idx // 512, idx % 128 // 32])


BF16 = ml_dtypes.bfloat16


def bf(x):
    return np.asarray(x, np.float32).astype(BF16)


def f64(x):
    return np.asarray(x).astype(np.float64)


B, H, N, P = 2, 1, 2048, 128
MASK_BIAS = 1.0e9
QS = 1.75 / np.sqrt(P)
KEEP = 0.75


def setup_inputs():
    s = mx_kscale(N)
    up = s.max() / s
    c = np.sqrt(2.0 * np.log(up))
    q = np.random.standard_normal((B, H, N, P)) * QS
    k = np.random.standard_normal((B, H, N, P)) * QS
    k[..., 0] += c
    v = np.random.standard_normal((B, H, N, P)) * 0.25 * up[:, None]
    mask = np.random.random((B, N)) < KEEP
    return {"q_s": bf(q), "k_s": bf(k), "v_s": bf(v), "mask": bf(mask)}


def reference(q_s, k_s, v_s, mask):
    diag_q = 0.5 * np.sum(f64(q_s) * f64(q_s), axis=-1)[..., :, None]
    diag_k = 0.5 * np.sum(f64(k_s) * f64(k_s), axis=-1)[..., None, :]
    product = (f64(q_s) @ f64(k_s).transpose(0, 1, 3, 2)
               - diag_q - diag_k
               - MASK_BIAS * (1.0 - f64(mask))[:, None, None, :])
    attn = np.exp(product)
    return mxq(attn, 3, "e4m3") @ mxq(f64(v_s), 2, "e4m3")

@@ -1,0 +1,231 @@
+from contextlib import ExitStack
+
+import concourse.mybir as mybir
+from concourse.masks import make_identity
+
+F32 = mybir.dt.float32
+BF16 = mybir.dt.bfloat16
+U32 = mybir.dt.uint32
+U8 = mybir.dt.uint8
+FP8X4 = mybir.dt.float8_e4m3fn_x4
+ALU = mybir.AluOpType
+ACT = mybir.ActivationFunctionType
+
+P = 128
+PACK = 4
+BATCH = 2
+TOKENS = 2048
+DIM = 128
+GROUP = P * PACK
+GROUPS = TOKENS // GROUP
+CHUNK = 512
+CHUNKS = TOKENS // CHUNK
+Q_TILES = CHUNK // P
+ALL_Q_TILES = TOKENS // P
+UNITS = BATCH * CHUNKS * GROUPS
+MASK_BIAS = 1.0e9
+RUN = 4
+
+TRANSPOSE_AHEAD = 3
+NORMS_AHEAD = 1
+QUANTISE_BEHIND = 2
+VALUES_BEHIND = 3
+STORE_BEHIND = 4
+
+FLOPS = 2 * (2 * BATCH * TOKENS * TOKENS * DIM)
+
+
+def unit_indices(u):
+    return u // (CHUNKS * GROUPS), (u // GROUPS) % CHUNKS, u % GROUPS
+
+
+def tile_softmaxattention_kde_pa_kernel(tc, q_s, k_s, v_s, mask, out):
+    nc = tc.nc
+    with ExitStack() as ctx:
+        ctx.enter_context(tc.manual_schedule())
+        keep = ctx.enter_context(tc.tile_pool(name="keep", bufs=1))
+        squares_pool = ctx.enter_context(tc.tile_pool(name="squares", bufs=3))
+        logits_pool = ctx.enter_context(tc.tile_pool(name="logits", bufs=3))
+        attn_pool = ctx.enter_context(tc.tile_pool(name="attn", bufs=4))
+        packed_pool = ctx.enter_context(tc.tile_pool(name="packed", bufs=2))
+        result_pool = ctx.enter_context(tc.tile_pool(name="result", bufs=2))
+        score_psum = ctx.enter_context(tc.psum_pool(name="score_psum", bufs=5))
+        prep_psum = ctx.enter_context(tc.psum_pool(name="prep_psum", bufs=2))
+        out_psum = ctx.enter_context(tc.psum_pool(name="out_psum", bufs=1))
+
+        raw = keep.tile([P, BATCH, GROUPS, 2, PACK, DIM], BF16)
+        flipped = keep.tile([P, BATCH, GROUPS, 2, CHUNK], BF16)
+        half_q_norm = keep.tile([P, BATCH, CHUNKS, CHUNK], F32)
+        key_bias = keep.tile([P, BATCH, GROUPS, PACK], F32)
+        mask_sb = keep.tile([P, BATCH * GROUPS, PACK], BF16)
+        mask_term = keep.tile([P, BATCH, GROUPS, PACK], F32)
+        v_sb = keep.tile([P, BATCH, GROUPS, PACK, DIM], BF16)
+        v_grouped = keep.tile([P, BATCH * GROUPS, DIM, PACK], BF16, align_bytes=64)
+        v_codes = keep.tile([P, BATCH * GROUPS, DIM], U32, align_bytes=64)
+        v_scales = keep.tile([P, BATCH * GROUPS, DIM], U8, align_bytes=64)
+        identity = keep.tile([P, P], BF16)
+        halves = keep.tile([P, P], F32)
+        warm = keep.tile([P, 1], F32)
+
+        def load_piece(b, i):
+            nc.sync.dma_start(
+                out=raw[:, b, i, 0, :, :],
+                in_=q_s[b, 0].rearrange("(j a) d -> j a d", a=ALL_Q_TILES)[:, i * Q_TILES : (i + 1) * Q_TILES, :],
+            )
+            nc.sync.dma_start(
+                out=raw[:, b, i, 1, :, :],
+                in_=k_s[b, 0, i * GROUP : (i + 1) * GROUP, :].rearrange("(p t) d -> p t d", t=PACK),
+            )
+
+        nc.scalar.dma_start(out=mask_sb[:], in_=mask.rearrange("b (g p t) -> p (b g) t", p=P, t=PACK))
+        load_piece(0, 0)
+        for b in range(BATCH):
+            nc.sync.dma_start(out=v_sb[:, b, :, :, :], in_=v_s[b, 0].rearrange("(g p t) d -> p g t d", p=P, t=PACK))
+        for b in range(BATCH):
+            for i in range(GROUPS):
+                if (b, i) != (0, 0):
+                    load_piece(b, i)
+
+        make_identity(nc, identity[:])
+        nc.vector.memset(warm[:], 0.0)
+        nc.vector.memset(halves[:], 0.5)
+        nc.scalar.activation(out=warm[:], in_=warm[:], func=ACT.Exp)
+        nc.vector.tensor_scalar(
+            out=mask_term[:].rearrange("p b g t -> p (b g) t"),
+            in0=mask_sb[:],
+            scalar1=-MASK_BIAS,
+            scalar2=MASK_BIAS,
+            op0=ALU.mult,
+            op1=ALU.add,
+        )
+
+        nc.vector.tensor_copy(out=v_grouped[:], in_=v_sb[:].rearrange("p b g t d -> p (b g) d t"))
+        nc.vector.quantize_mx(
+            out=v_codes[:].rearrange("p s d -> p (s d)").bitcast(FP8X4),
+            scales=v_scales[:].rearrange("p s d -> p (s d)"),
+            in_=v_grouped[:].rearrange("p s d t -> p (s d t)"),
+        )
+
+        squares = {}
+        logits = {}
+        attn = {}
+        packed = {}
+        sums = {}
+
+        def transpose_piece(b, i):
+            turned = prep_psum.tile([P, 2, PACK, P], BF16, tag="prep")
+            for side in range(2):
+                for a in range(PACK):
+                    nc.tensor.transpose(turned[:, side, a, :], raw[:, b, i, side, a, :], identity[:])
+            nc.scalar.copy(out=flipped[:, b, i, :, :], in_=turned[:].rearrange("p s a j -> p s (a j)"))
+            squared = squares_pool.tile([P, 2, CHUNK], F32)
+            nc.gpsimd.tensor_tensor(out=squared[:], in0=flipped[:, b, i, :, :], in1=flipped[:, b, i, :, :], op=ALU.mult)
+            squares[(b, i)] = squared
+
+        def norms_of_piece(b, i):
+            squared = squares[(b, i)]
+            q_rows = prep_psum.tile([P, CHUNK], F32, tag="prep")
+            nc.tensor.matmul(out=q_rows[:], lhsT=halves[:], rhs=squared[:, 0, :], start=True, stop=True)
+            nc.scalar.copy(out=half_q_norm[:, b, i, :], in_=q_rows[:])
+            k_cols = prep_psum.tile([P, PACK], F32, tag="prep")
+            for t in range(PACK):
+                nc.tensor.matmul(
+                    out=k_cols[:, t : t + 1],
+                    lhsT=squared[:, 1, t * P : (t + 1) * P],
+                    rhs=halves[:, 0:1],
+                    start=True,
+                    stop=True,
+                )
+            nc.vector.tensor_tensor(out=key_bias[:, b, i, :], in0=k_cols[:], in1=mask_term[:, b, i, :], op=ALU.add)
+
+        def scores_to_logits(u):
+            b, c, g = unit_indices(u)
+            unit_logits = logits_pool.tile([P, PACK, CHUNK], F32)
+            for t in range(PACK):
+                scores = score_psum.tile([P, CHUNK], F32)
+                nc.tensor.matmul(
+                    out=scores[:],
+                    lhsT=flipped[:, b, g, 1, t * P : (t + 1) * P],
+                    rhs=flipped[:, b, c, 0, :],
+                    start=True,
+                    stop=True,
+                )
+                nc.vector.scalar_tensor_tensor(
+                    out=unit_logits[:, t, :],
+                    in0=scores[:],
+                    scalar=key_bias[:, b, g, t : t + 1],
+                    in1=half_q_norm[:, b, c, :],
+                    op0=ALU.subtract,
+                    op1=ALU.subtract,
+                )
+            logits[u] = unit_logits
+
+        def exponentials(u):
+            unit_attn = attn_pool.tile([P, CHUNK, PACK], BF16, align_bytes=64)
+            nc.scalar.activation(
+                out=unit_attn[:].rearrange("p (c i) t -> p c t i", i=RUN),
+                in_=logits[u][:].rearrange("p t (c i) -> p c t i", i=RUN),
+                func=ACT.Exp,
+            )
+            attn[u] = unit_attn
+
+        def quantise(u):
+            b, c, g = unit_indices(u)
+            if g == 0:
+                codes = packed_pool.tile([P, GROUPS, CHUNK], U32, align_bytes=64)
+                scales = packed_pool.tile([P, GROUPS, CHUNK], U8, align_bytes=64)
+                packed[(b, c)] = (codes, scales)
+            codes, scales = packed[(b, c)]
+            nc.vector.quantize_mx(
+                out=codes[:, g, :].bitcast(FP8X4),
+                scales=scales[:, g, :],
+                in_=attn[u][:].rearrange("p n t -> p (n t)"),
+            )
+
+        def attn_times_values(b, c):
+            codes, scales = packed[(b, c)]
+            acc = out_psum.tile([P, Q_TILES, DIM], F32)
+            for a in range(Q_TILES):
+                queries = slice(a * P, (a + 1) * P)
+                for g in range(GROUPS):
+                    nc.tensor.matmul_mx(
+                        out=acc[:, a, :],
+                        lhsT=codes[:, g, queries].bitcast(FP8X4),
+                        lhsT_scale=scales[:, g, queries],
+                        rhs=v_codes[:, b * GROUPS + g, :].bitcast(FP8X4),
+                        rhs_scale=v_scales[:, b * GROUPS + g, :],
+                        start=(g == 0),
+                        stop=(g == GROUPS - 1),
+                    )
+            sums[(b, c)] = acc
+
+        def store(b, c):
+            result = result_pool.tile([P, Q_TILES, DIM], F32)
+            nc.scalar.copy(out=result[:], in_=sums[(b, c)][:])
+            nc.sync.dma_start(
+                out=out[b, 0].rearrange("(j a) d -> j a d", a=ALL_Q_TILES)[:, c * Q_TILES : (c + 1) * Q_TILES, :],
+                in_=result[:],
+            )
+
+        def is_unit(u):
+            return 0 <= u < UNITS
+
+        for step in range(-TRANSPOSE_AHEAD, UNITS + STORE_BEHIND + 1):
+            ahead = step + TRANSPOSE_AHEAD
+            if is_unit(ahead) and unit_indices(ahead)[1] == 0:
+                transpose_piece(unit_indices(ahead)[0], unit_indices(ahead)[2])
+            if is_unit(step):
+                scores_to_logits(step)
+            ahead = step + NORMS_AHEAD
+            if is_unit(ahead) and unit_indices(ahead)[1] == 0:
+                norms_of_piece(unit_indices(ahead)[0], unit_indices(ahead)[2])
+            behind = step - VALUES_BEHIND
+            if is_unit(behind) and unit_indices(behind)[2] == GROUPS - 1:
+                attn_times_values(unit_indices(behind)[0], unit_indices(behind)[1])
+            behind = step - STORE_BEHIND
+            if is_unit(behind) and unit_indices(behind)[2] == GROUPS - 1:
+                store(unit_indices(behind)[0], unit_indices(behind)[1])
+            if is_unit(step - QUANTISE_BEHIND):
+                quantise(step - QUANTISE_BEHIND)
+            if is_unit(step):
+                exponentials(step)

@@ -26,7 +26,7 @@ UNITS = BATCH * CHUNKS * GROUPS
 MASK_BIAS = 1.0e9
 RUN = 4
 
-TRANSPOSE_AHEAD = 3
+FLIP_AHEAD = 3
 NORMS_AHEAD = 1
 QUANTISE_BEHIND = 2
 VALUES_BEHIND = 3
@@ -44,7 +44,7 @@ def tile_softmaxattention_kde_pa_kernel(tc, q_s, k_s, v_s, mask, out):
     with ExitStack() as ctx:
         ctx.enter_context(tc.manual_schedule())
         keep = ctx.enter_context(tc.tile_pool(name="keep", bufs=1))
-        squares_pool = ctx.enter_context(tc.tile_pool(name="squares", bufs=3))
+        squares_pool = ctx.enter_context(tc.tile_pool(name="squares", bufs=4))
         logits_pool = ctx.enter_context(tc.tile_pool(name="logits", bufs=3))
         attn_pool = ctx.enter_context(tc.tile_pool(name="attn", bufs=4))
         packed_pool = ctx.enter_context(tc.tile_pool(name="packed", bufs=2))
@@ -53,8 +53,10 @@ def tile_softmaxattention_kde_pa_kernel(tc, q_s, k_s, v_s, mask, out):
         prep_psum = ctx.enter_context(tc.psum_pool(name="prep_psum", bufs=2))
         out_psum = ctx.enter_context(tc.psum_pool(name="out_psum", bufs=1))
 
-        raw = keep.tile([P, BATCH, GROUPS, 2, PACK, DIM], BF16)
-        flipped = keep.tile([P, BATCH, GROUPS, 2, CHUNK], BF16)
+        q_raw = keep.tile([P, BATCH, CHUNKS, Q_TILES, DIM], BF16)
+        k_raw = keep.tile([P, BATCH, GROUPS, PACK, DIM], BF16)
+        q_flipped = keep.tile([P, BATCH, CHUNKS, CHUNK], BF16)
+        k_flipped = keep.tile([P, BATCH, GROUPS, GROUP], BF16)
         half_q_norm = keep.tile([P, BATCH, CHUNKS, CHUNK], F32)
         key_bias = keep.tile([P, BATCH, GROUPS, PACK], F32)
         mask_sb = keep.tile([P, BATCH * GROUPS, PACK], BF16)
@@ -67,24 +69,30 @@ def tile_softmaxattention_kde_pa_kernel(tc, q_s, k_s, v_s, mask, out):
         halves = keep.tile([P, P], F32)
         warm = keep.tile([P, 1], F32)
 
-        def load_piece(b, i):
+        def load_queries(b, c):
             nc.sync.dma_start(
-                out=raw[:, b, i, 0, :, :],
-                in_=q_s[b, 0].rearrange("(j a) d -> j a d", a=ALL_Q_TILES)[:, i * Q_TILES : (i + 1) * Q_TILES, :],
+                out=q_raw[:, b, c, :, :],
+                in_=q_s[b, 0].rearrange("(j a) d -> j a d", a=ALL_Q_TILES)[:, c * Q_TILES : (c + 1) * Q_TILES, :],
             )
+
+        def load_keys(b, g):
             nc.sync.dma_start(
-                out=raw[:, b, i, 1, :, :],
-                in_=k_s[b, 0, i * GROUP : (i + 1) * GROUP, :].rearrange("(p t) d -> p t d", t=PACK),
+                out=k_raw[:, b, g, :, :],
+                in_=k_s[b, 0, g * GROUP : (g + 1) * GROUP, :].rearrange("(p t) d -> p t d", t=PACK),
             )
 
         nc.scalar.dma_start(out=mask_sb[:], in_=mask.rearrange("b (g p t) -> p (b g) t", p=P, t=PACK))
-        load_piece(0, 0)
+        load_queries(0, 0)
+        load_keys(0, 0)
         for b in range(BATCH):
             nc.sync.dma_start(out=v_sb[:, b, :, :, :], in_=v_s[b, 0].rearrange("(g p t) d -> p g t d", p=P, t=PACK))
         for b in range(BATCH):
-            for i in range(GROUPS):
-                if (b, i) != (0, 0):
-                    load_piece(b, i)
+            for g in range(GROUPS):
+                if (b, g) != (0, 0):
+                    load_keys(b, g)
+            for c in range(CHUNKS):
+                if (b, c) != (0, 0):
+                    load_queries(b, c)
 
         make_identity(nc, identity[:])
         nc.vector.memset(warm[:], 0.0)
@@ -106,37 +114,38 @@ def tile_softmaxattention_kde_pa_kernel(tc, q_s, k_s, v_s, mask, out):
             in_=v_grouped[:].rearrange("p s d t -> p (s d t)"),
         )
 
-        squares = {}
+        q_squares = {}
+        k_squares = {}
         logits = {}
         attn = {}
         packed = {}
         sums = {}
 
-        def transpose_piece(b, i):
-            turned = prep_psum.tile([P, 2, PACK, P], BF16, tag="prep")
-            for side in range(2):
-                for a in range(PACK):
-                    nc.tensor.transpose(turned[:, side, a, :], raw[:, b, i, side, a, :], identity[:])
-            nc.scalar.copy(out=flipped[:, b, i, :, :], in_=turned[:].rearrange("p s a j -> p s (a j)"))
-            squared = squares_pool.tile([P, 2, CHUNK], F32)
-            nc.gpsimd.tensor_tensor(out=squared[:], in0=flipped[:, b, i, :, :], in1=flipped[:, b, i, :, :], op=ALU.mult)
-            squares[(b, i)] = squared
+        def flip(tokens, features):
+            turned = prep_psum.tile([P, PACK, P], BF16, tag="prep")
+            for a in range(PACK):
+                nc.tensor.transpose(turned[:, a, :], tokens[:, a, :], identity[:])
+            nc.scalar.copy(out=features, in_=turned[:].rearrange("p a j -> p (a j)"))
+            squared = squares_pool.tile([P, PACK * P], F32)
+            nc.gpsimd.tensor_tensor(out=squared[:], in0=features, in1=features, op=ALU.mult)
+            return squared
 
-        def norms_of_piece(b, i):
-            squared = squares[(b, i)]
+        def query_norms(b, c):
             q_rows = prep_psum.tile([P, CHUNK], F32, tag="prep")
-            nc.tensor.matmul(out=q_rows[:], lhsT=halves[:], rhs=squared[:, 0, :], start=True, stop=True)
-            nc.scalar.copy(out=half_q_norm[:, b, i, :], in_=q_rows[:])
+            nc.tensor.matmul(out=q_rows[:], lhsT=halves[:], rhs=q_squares[(b, c)][:], start=True, stop=True)
+            nc.scalar.copy(out=half_q_norm[:, b, c, :], in_=q_rows[:])
+
+        def key_norms(b, g):
             k_cols = prep_psum.tile([P, PACK], F32, tag="prep")
             for t in range(PACK):
                 nc.tensor.matmul(
                     out=k_cols[:, t : t + 1],
-                    lhsT=squared[:, 1, t * P : (t + 1) * P],
+                    lhsT=k_squares[(b, g)][:, t * P : (t + 1) * P],
                     rhs=halves[:, 0:1],
                     start=True,
                     stop=True,
                 )
-            nc.vector.tensor_tensor(out=key_bias[:, b, i, :], in0=k_cols[:], in1=mask_term[:, b, i, :], op=ALU.add)
+            nc.vector.tensor_tensor(out=key_bias[:, b, g, :], in0=k_cols[:], in1=mask_term[:, b, g, :], op=ALU.add)
 
         def scores_to_logits(u):
             b, c, g = unit_indices(u)
@@ -145,8 +154,8 @@ def tile_softmaxattention_kde_pa_kernel(tc, q_s, k_s, v_s, mask, out):
                 scores = score_psum.tile([P, CHUNK], F32)
                 nc.tensor.matmul(
                     out=scores[:],
-                    lhsT=flipped[:, b, g, 1, t * P : (t + 1) * P],
-                    rhs=flipped[:, b, c, 0, :],
+                    lhsT=k_flipped[:, b, g, t * P : (t + 1) * P],
+                    rhs=q_flipped[:, b, c, :],
                     start=True,
                     stop=True,
                 )
@@ -210,15 +219,21 @@ def tile_softmaxattention_kde_pa_kernel(tc, q_s, k_s, v_s, mask, out):
         def is_unit(u):
             return 0 <= u < UNITS
 
-        for step in range(-TRANSPOSE_AHEAD, UNITS + STORE_BEHIND + 1):
-            ahead = step + TRANSPOSE_AHEAD
-            if is_unit(ahead) and unit_indices(ahead)[1] == 0:
-                transpose_piece(unit_indices(ahead)[0], unit_indices(ahead)[2])
+        for step in range(-FLIP_AHEAD, UNITS + STORE_BEHIND + 1):
+            if is_unit(step + FLIP_AHEAD):
+                b, c, g = unit_indices(step + FLIP_AHEAD)
+                if g == 0:
+                    q_squares[(b, c)] = flip(q_raw[:, b, c, :, :], q_flipped[:, b, c, :])
+                if c == 0:
+                    k_squares[(b, g)] = flip(k_raw[:, b, g, :, :], k_flipped[:, b, g, :])
             if is_unit(step):
                 scores_to_logits(step)
-            ahead = step + NORMS_AHEAD
-            if is_unit(ahead) and unit_indices(ahead)[1] == 0:
-                norms_of_piece(unit_indices(ahead)[0], unit_indices(ahead)[2])
+            if is_unit(step + NORMS_AHEAD):
+                b, c, g = unit_indices(step + NORMS_AHEAD)
+                if g == 0:
+                    query_norms(b, c)
+                if c == 0:
+                    key_norms(b, g)
             behind = step - VALUES_BEHIND
             if is_unit(behind) and unit_indices(behind)[2] == GROUPS - 1:
                 attn_times_values(unit_indices(behind)[0], unit_indices(behind)[1])

@@ -125,9 +125,9 @@ def tile_softmaxattention_kde_pa_kernel(tc, q_s, k_s, v_s, mask, out):
             turned = prep_psum.tile([P, PACK, P], BF16, tag="prep")
             for a in range(PACK):
                 nc.tensor.transpose(turned[:, a, :], tokens[:, a, :], identity[:])
-            nc.scalar.copy(out=features, in_=turned[:].rearrange("p a j -> p (a j)"))
             squared = squares_pool.tile([P, PACK * P], F32)
-            nc.gpsimd.tensor_tensor(out=squared[:], in0=features, in1=features, op=ALU.mult)
+            nc.scalar.activation(out=squared[:], in_=turned[:].rearrange("p a j -> p (a j)"), func=ACT.Square)
+            nc.scalar.copy(out=features, in_=turned[:].rearrange("p a j -> p (a j)"))
             return squared
 
         def query_norms(b, c):

@@ -42,7 +42,6 @@ def unit_indices(u):
 def tile_softmaxattention_kde_pa_kernel(tc, q_s, k_s, v_s, mask, out):
     nc = tc.nc
     with ExitStack() as ctx:
-        ctx.enter_context(tc.manual_schedule())
         keep = ctx.enter_context(tc.tile_pool(name="keep", bufs=1))
         squares_pool = ctx.enter_context(tc.tile_pool(name="squares", bufs=4))
         logits_pool = ctx.enter_context(tc.tile_pool(name="logits", bufs=3))
@@ -125,9 +124,9 @@ def tile_softmaxattention_kde_pa_kernel(tc, q_s, k_s, v_s, mask, out):
             turned = prep_psum.tile([P, PACK, P], BF16, tag="prep")
             for a in range(PACK):
                 nc.tensor.transpose(turned[:, a, :], tokens[:, a, :], identity[:])
-            squared = squares_pool.tile([P, PACK * P], F32)
-            nc.scalar.activation(out=squared[:], in_=turned[:].rearrange("p a j -> p (a j)"), func=ACT.Square)
             nc.scalar.copy(out=features, in_=turned[:].rearrange("p a j -> p (a j)"))
+            squared = squares_pool.tile([P, PACK * P], F32)
+            nc.gpsimd.tensor_tensor(out=squared[:], in0=features, in1=features, op=ALU.mult)
             return squared
 
         def query_norms(b, c):

@@ -26,11 +26,8 @@ UNITS = BATCH * CHUNKS * GROUPS
 MASK_BIAS = 1.0e9
 RUN = 4
 
-FLIP_AHEAD = 3
-NORMS_AHEAD = 1
-QUANTISE_BEHIND = 2
-VALUES_BEHIND = 3
-STORE_BEHIND = 4
+FOLD_GROUP = GROUPS - 1
+PARTS = 3
 
 FLOPS = 2 * (2 * BATCH * TOKENS * TOKENS * DIM)
 
@@ -39,33 +36,48 @@ def unit_indices(u):
     return u // (CHUNKS * GROUPS), (u // GROUPS) % CHUNKS, u % GROUPS
 
 
+def folded_tiles(b, c):
+    return 2 - c % 2
+
+
 def tile_softmaxattention_kde_pa_kernel(tc, q_s, k_s, v_s, mask, out):
     nc = tc.nc
     with ExitStack() as ctx:
         keep = ctx.enter_context(tc.tile_pool(name="keep", bufs=1))
         squares_pool = ctx.enter_context(tc.tile_pool(name="squares", bufs=4))
+        rest_pool = ctx.enter_context(tc.tile_pool(name="rest", bufs=4))
+        unused_pool = ctx.enter_context(tc.tile_pool(name="unused", bufs=4))
         logits_pool = ctx.enter_context(tc.tile_pool(name="logits", bufs=3))
-        attn_pool = ctx.enter_context(tc.tile_pool(name="attn", bufs=4))
+        attn_pool = ctx.enter_context(tc.tile_pool(name="attn", bufs=3))
         packed_pool = ctx.enter_context(tc.tile_pool(name="packed", bufs=2))
-        result_pool = ctx.enter_context(tc.tile_pool(name="result", bufs=2))
+        result_pool = ctx.enter_context(tc.tile_pool(name="result", bufs=4))
         score_psum = ctx.enter_context(tc.psum_pool(name="score_psum", bufs=5))
         prep_psum = ctx.enter_context(tc.psum_pool(name="prep_psum", bufs=2))
         out_psum = ctx.enter_context(tc.psum_pool(name="out_psum", bufs=1))
+        ctx.enter_context(tc.manual_schedule())
 
         q_raw = keep.tile([P, BATCH, CHUNKS, Q_TILES, DIM], BF16)
         k_raw = keep.tile([P, BATCH, GROUPS, PACK, DIM], BF16)
         q_flipped = keep.tile([P, BATCH, CHUNKS, CHUNK], BF16)
         k_flipped = keep.tile([P, BATCH, GROUPS, GROUP], BF16)
-        half_q_norm = keep.tile([P, BATCH, CHUNKS, CHUNK], F32)
-        key_bias = keep.tile([P, BATCH, GROUPS, PACK], F32)
+        q_square = keep.tile([P, BATCH, CHUNKS, Q_TILES], F32)
+        k_square = keep.tile([P, BATCH, GROUPS, PACK], F32)
+        k_terms = keep.tile([P, BATCH, PACK, P], BF16)
+        q_terms = keep.tile([P, 2, Q_TILES, P], BF16)
+        k_folds = keep.tile([P, BATCH, PACK, P], BF16)
+        q_folds = keep.tile([P, BATCH, CHUNKS, Q_TILES, P], BF16)
+        q_column = keep.tile([P, BATCH, CHUNKS, Q_TILES], F32)
+        q_row = keep.tile([P, BATCH, CHUNKS, CHUNK], F32)
+        k_column = keep.tile([P, BATCH, GROUPS, PACK], F32)
         mask_sb = keep.tile([P, BATCH * GROUPS, PACK], BF16)
         mask_term = keep.tile([P, BATCH, GROUPS, PACK], F32)
         v_sb = keep.tile([P, BATCH, GROUPS, PACK, DIM], BF16)
-        v_grouped = keep.tile([P, BATCH * GROUPS, DIM, PACK], BF16, align_bytes=64)
-        v_codes = keep.tile([P, BATCH * GROUPS, DIM], U32, align_bytes=64)
-        v_scales = keep.tile([P, BATCH * GROUPS, DIM], U8, align_bytes=64)
+        v_grouped = keep.tile([P, BATCH, GROUPS, DIM, PACK], BF16, align_bytes=64)
+        v_codes = keep.tile([P, BATCH, GROUPS, DIM], U32, align_bytes=64)
+        v_scales = keep.tile([P, BATCH, GROUPS, DIM], U8, align_bytes=64)
         identity = keep.tile([P, P], BF16)
-        halves = keep.tile([P, P], F32)
+        identity_f32 = keep.tile([P, P], F32)
+        minus_half = keep.tile([P, 1], F32)
         warm = keep.tile([P, 1], F32)
 
         def load_queries(b, c):
@@ -81,165 +93,394 @@ def tile_softmaxattention_kde_pa_kernel(tc, q_s, k_s, v_s, mask, out):
             )
 
         nc.scalar.dma_start(out=mask_sb[:], in_=mask.rearrange("b (g p t) -> p (b g) t", p=P, t=PACK))
-        load_queries(0, 0)
-        load_keys(0, 0)
         for b in range(BATCH):
-            nc.sync.dma_start(out=v_sb[:, b, :, :, :], in_=v_s[b, 0].rearrange("(g p t) d -> p g t d", p=P, t=PACK))
-        for b in range(BATCH):
+            load_queries(b, 0)
             for g in range(GROUPS):
-                if (b, g) != (0, 0):
-                    load_keys(b, g)
-            for c in range(CHUNKS):
-                if (b, c) != (0, 0):
-                    load_queries(b, c)
+                load_keys(b, g)
+            load_queries(b, 1)
+            nc.sync.dma_start(out=v_sb[:, b, :, :, :], in_=v_s[b, 0].rearrange("(g p t) d -> p g t d", p=P, t=PACK))
+            for c in range(2, CHUNKS):
+                load_queries(b, c)
 
         make_identity(nc, identity[:])
+        make_identity(nc, identity_f32[:])
         nc.vector.memset(warm[:], 0.0)
-        nc.vector.memset(halves[:], 0.5)
+        nc.vector.memset(minus_half[:], -0.5)
         nc.scalar.activation(out=warm[:], in_=warm[:], func=ACT.Exp)
-        nc.vector.tensor_scalar(
+        nc.gpsimd.tensor_scalar(
             out=mask_term[:].rearrange("p b g t -> p (b g) t"),
             in0=mask_sb[:],
-            scalar1=-MASK_BIAS,
-            scalar2=MASK_BIAS,
+            scalar1=MASK_BIAS,
+            scalar2=-MASK_BIAS,
             op0=ALU.mult,
             op1=ALU.add,
         )
 
-        nc.vector.tensor_copy(out=v_grouped[:], in_=v_sb[:].rearrange("p b g t d -> p (b g) d t"))
-        nc.vector.quantize_mx(
-            out=v_codes[:].rearrange("p s d -> p (s d)").bitcast(FP8X4),
-            scales=v_scales[:].rearrange("p s d -> p (s d)"),
-            in_=v_grouped[:].rearrange("p s d t -> p (s d t)"),
-        )
+        prep = {}
+        for terms, first_one in ((k_terms, PARTS), (q_terms, 0)):
+            nc.gpsimd.memset(terms[:], 0.0)
+            nc.gpsimd.memset(terms[:, :, :, first_one : first_one + PARTS], 1.0)
 
-        q_squares = {}
-        k_squares = {}
+        squares = {}
         logits = {}
         attn = {}
         packed = {}
         sums = {}
 
-        def flip(tokens, features):
+        q0, k0, k1, k2, k3 = [("q", 0, 0)] + [("k", 0, g) for g in range(GROUPS)]
+
+        def raw(block):
+            kind, b, n = block
+            return q_raw[:, b, n, :, :] if kind == "q" else k_raw[:, b, n, :, :]
+
+        def flipped(block):
+            kind, b, n = block
+            return q_flipped[:, b, n, :] if kind == "q" else k_flipped[:, b, n, :]
+
+        def flip(block):
             turned = prep_psum.tile([P, PACK, P], BF16, tag="prep")
             for a in range(PACK):
-                nc.tensor.transpose(turned[:, a, :], tokens[:, a, :], identity[:])
-            nc.scalar.copy(out=features, in_=turned[:].rearrange("p a j -> p (a j)"))
+                nc.tensor.transpose(turned[:, a, :], raw(block)[:, a, :], identity[:])
+            prep[("flip", block)] = turned[:].rearrange("p a j -> p (a j)")
+
+        def flip_out(block, engine_copy=nc.scalar.copy):
+            engine_copy(out=flipped(block), in_=prep[("flip", block)])
+
+        def square(block):
             squared = squares_pool.tile([P, PACK * P], F32)
-            nc.gpsimd.tensor_tensor(out=squared[:], in0=features, in1=features, op=ALU.mult)
-            return squared
+            nc.gpsimd.tensor_tensor(out=squared[:], in0=flipped(block), in1=flipped(block), op=ALU.mult)
+            squares[block] = squared
 
-        def query_norms(b, c):
-            q_rows = prep_psum.tile([P, CHUNK], F32, tag="prep")
-            nc.tensor.matmul(out=q_rows[:], lhsT=halves[:], rhs=q_squares[(b, c)][:], start=True, stop=True)
-            nc.scalar.copy(out=half_q_norm[:, b, c, :], in_=q_rows[:])
-
-        def key_norms(b, g):
-            k_cols = prep_psum.tile([P, PACK], F32, tag="prep")
-            for t in range(PACK):
-                nc.tensor.matmul(
-                    out=k_cols[:, t : t + 1],
-                    lhsT=k_squares[(b, g)][:, t * P : (t + 1) * P],
-                    rhs=halves[:, 0:1],
-                    start=True,
-                    stop=True,
-                )
-            nc.vector.tensor_tensor(out=key_bias[:, b, g, :], in0=k_cols[:], in1=mask_term[:, b, g, :], op=ALU.add)
-
-        def scores_to_logits(u):
-            b, c, g = unit_indices(u)
-            unit_logits = logits_pool.tile([P, PACK, CHUNK], F32)
-            for t in range(PACK):
-                scores = score_psum.tile([P, CHUNK], F32)
-                nc.tensor.matmul(
-                    out=scores[:],
-                    lhsT=k_flipped[:, b, g, t * P : (t + 1) * P],
-                    rhs=q_flipped[:, b, c, :],
-                    start=True,
-                    stop=True,
-                )
+        def query_bias_by_vector(block):
+            kind, b, n = block
+            for a in range(Q_TILES):
+                unused = unused_pool.tile([P, DIM], F32)
                 nc.vector.scalar_tensor_tensor(
-                    out=unit_logits[:, t, :],
-                    in0=scores[:],
-                    scalar=key_bias[:, b, g, t : t + 1],
-                    in1=half_q_norm[:, b, c, :],
-                    op0=ALU.subtract,
-                    op1=ALU.subtract,
+                    out=unused[:],
+                    in0=raw(block)[:, a, :],
+                    scalar=-0.5,
+                    in1=raw(block)[:, a, :],
+                    op0=ALU.mult,
+                    op1=ALU.mult,
+                    accum_out=q_column[:, b, n, a : a + 1],
                 )
-            logits[u] = unit_logits
 
-        def exponentials(u):
-            unit_attn = attn_pool.tile([P, CHUNK, PACK], BF16, align_bytes=64)
+        def squares_by_scalar(block):
+            kind, b, n = block
+            total = q_square if kind == "q" else k_square
+            for t in range(PACK):
+                unused = unused_pool.tile([P, DIM], F32)
+                nc.scalar.activation(
+                    out=unused[:], in_=raw(block)[:, t, :], func=ACT.Square, accum_out=total[:, b, n, t : t + 1]
+                )
+
+        def bias_from_squares(block):
+            kind, b, n = block
+            if kind == "q":
+                nc.vector.tensor_scalar(
+                    out=q_column[:, b, n, :], in0=q_square[:, b, n, :], scalar1=-0.5, scalar2=None, op0=ALU.mult
+                )
+            else:
+                nc.vector.scalar_tensor_tensor(
+                    out=k_column[:, b, n, :],
+                    in0=k_square[:, b, n, :],
+                    scalar=-0.5,
+                    in1=mask_term[:, b, n, :],
+                    op0=ALU.mult,
+                    op1=ALU.add,
+                )
+
+        def norm(block):
+            columns = prep_psum.tile([P, PACK], F32, tag="prep")
+            for t in range(PACK):
+                nc.tensor.matmul(
+                    out=columns[:, t : t + 1],
+                    lhsT=squares[block][:, t * P : (t + 1) * P],
+                    rhs=minus_half[:],
+                    start=True,
+                    stop=True,
+                )
+            prep[("norm", block)] = columns[:]
+
+        def norm_out(block):
+            kind, b, n = block
+            columns = prep[("norm", block)]
+            if kind == "q":
+                nc.scalar.copy(out=q_column[:, b, n, :], in_=columns)
+            else:
+                nc.vector.tensor_tensor(out=k_column[:, b, n, :], in0=columns, in1=mask_term[:, b, n, :], op=ALU.add)
+
+        def terms_of(block):
+            kind, b, n = block
+            if kind == "k":
+                return k_column[:, b, n, :], k_terms[:, b, :, 0:PARTS], k_terms[:, b, :, :], k_folds[:, b, :, :]
+            tiles = slice(Q_TILES - folded_tiles(b, n), Q_TILES)
+            return (
+                q_column[:, b, n, tiles],
+                q_terms[:, n % 2, tiles, PARTS : 2 * PARTS],
+                q_terms[:, n % 2, tiles, :],
+                q_folds[:, b, n, tiles, :],
+            )
+
+        def split(block):
+            left, parts = terms_of(block)[:2]
+            for part in range(PARTS):
+                nc.gpsimd.tensor_copy(out=parts[:, :, part], in_=left)
+                if part + 1 < PARTS:
+                    rest = rest_pool.tile([P, PACK], F32, name="rest")[:, 0 : left.shape[1]]
+                    nc.gpsimd.tensor_tensor(out=rest, in0=left, in1=parts[:, :, part], op=ALU.subtract)
+                    left = rest
+
+        def fold_flip(block):
+            terms = terms_of(block)[2]
+            turned = prep_psum.tile([P, PACK, P], BF16, tag="prep", name="turned_terms")
+            tiles = terms.shape[1]
+            for t in range(tiles):
+                nc.tensor.transpose(turned[:, t, :], terms[:, t, :], identity[:])
+            prep[("fold", block)] = turned[:, 0:tiles, :]
+
+        def fold_out(block):
+            nc.scalar.copy(out=terms_of(block)[3], in_=prep[("fold", block)])
+
+        def row(block):
+            kind, b, c = block
+            rows = (score_psum if block == q0 else prep_psum).tile([P, Q_TILES, P], F32, tag="scores" if block == q0 else "prep", name="rows")
+            for a in range(Q_TILES):
+                nc.tensor.transpose(rows[:, a, :], q_column[:, b, c, a : a + 1].to_broadcast([P, P]), identity_f32[:])
+            prep[("row", block)] = rows[:].rearrange("p a n -> p (a n)")
+
+        def row_out(block):
+            kind, b, c = block
+            nc.scalar.copy(out=q_row[:, b, c, :], in_=prep[("row", block)])
+
+        def subtracted_queries(u):
+            b, c, g = unit_indices(u)
+            return CHUNK - (folded_tiles(b, c) * P if g == FOLD_GROUP else 0)
+
+        def scores_to_logits(u, t):
+            b, c, g = unit_indices(u)
+            queries = subtracted_queries(u)
+            if t == 0:
+                logits[u] = logits_pool.tile([P, PACK, CHUNK], F32, name="unit_logits")
+            scores = score_psum.tile([P, CHUNK], F32, tag="scores")
+            nc.tensor.matmul(
+                out=scores[:, 0:queries],
+                lhsT=k_flipped[:, b, g, t * P : (t + 1) * P],
+                rhs=q_flipped[:, b, c, 0:queries],
+                start=True,
+                stop=True,
+            )
+            nc.vector.scalar_tensor_tensor(
+                out=logits[u][:, t, 0:queries],
+                in0=scores[:, 0:queries],
+                scalar=k_column[:, b, g, t : t + 1],
+                in1=q_row[:, b, c, 0:queries],
+                op0=ALU.add,
+                op1=ALU.add,
+            )
+
+        def folded_tile(u, a):
+            b, c, g = unit_indices(u)
+            queries = slice(a * P, (a + 1) * P)
+            bank = score_psum.tile([P, PACK, P], F32, tag="scores", name="bank")
+            for t in range(PACK):
+                nc.tensor.matmul(
+                    out=bank[:, t, :],
+                    lhsT=k_flipped[:, b, g, t * P : (t + 1) * P],
+                    rhs=q_flipped[:, b, c, queries],
+                    start=True,
+                    stop=False,
+                )
+                nc.tensor.matmul(
+                    out=bank[:, t, :],
+                    lhsT=k_folds[:, b, t, :],
+                    rhs=q_folds[:, b, c, a, :],
+                    start=False,
+                    stop=True,
+                )
             nc.scalar.activation(
-                out=unit_attn[:].rearrange("p (c i) t -> p c t i", i=RUN),
-                in_=logits[u][:].rearrange("p t (c i) -> p c t i", i=RUN),
+                out=attn_of(u)[:, queries, :],
+                in_=bank[:].rearrange("p t n -> p n t"),
                 func=ACT.Exp,
             )
-            attn[u] = unit_attn
 
-        def quantise(u):
-            b, c, g = unit_indices(u)
-            if g == 0:
+        def attn_of(u):
+            if u // 2 not in attn:
+                attn[u // 2] = attn_pool.tile([P, 2, CHUNK, PACK], BF16, align_bytes=64, name="pair_attn")
+            return attn[u // 2][:, u % 2, :, :]
+
+        def exponentials(u, start, stop):
+            queries = slice(start, stop)
+            nc.scalar.activation(
+                out=attn_of(u)[:, queries, :].rearrange("p (c i) t -> p c t i", i=RUN),
+                in_=logits[u][:, :, queries].rearrange("p t (c i) -> p c t i", i=RUN),
+                func=ACT.Exp,
+            )
+
+        def group_values(b):
+            for g in range(GROUPS):
+                nc.gpsimd.tensor_scalar(
+                    out=v_grouped[:, b, g, :, :],
+                    in0=v_sb[:, b, g, :, :].rearrange("p t d -> p d t"),
+                    scalar1=1.0,
+                    scalar2=0.0,
+                    op0=ALU.mult,
+                    op1=ALU.add,
+                )
+
+        def quantise_values(b):
+            nc.vector.quantize_mx(
+                out=v_codes[:, b, :, :].rearrange("p g d -> p (g d)").bitcast(FP8X4),
+                scales=v_scales[:, b, :, :].rearrange("p g d -> p (g d)"),
+                in_=v_grouped[:, b, :, :, :].rearrange("p g d t -> p (g d t)"),
+            )
+
+        def packed_of(b, c):
+            if (b, c) not in packed:
                 codes = packed_pool.tile([P, GROUPS, CHUNK], U32, align_bytes=64)
                 scales = packed_pool.tile([P, GROUPS, CHUNK], U8, align_bytes=64)
                 packed[(b, c)] = (codes, scales)
-            codes, scales = packed[(b, c)]
+            return packed[(b, c)]
+
+        def quantise_pair(u):
+            b, c, g = unit_indices(u)
+            codes, scales = packed_of(b, c)
             nc.vector.quantize_mx(
-                out=codes[:, g, :].bitcast(FP8X4),
-                scales=scales[:, g, :],
-                in_=attn[u][:].rearrange("p n t -> p (n t)"),
+                out=codes[:, g - 1 : g + 1, :].rearrange("p g n -> p (g n)").bitcast(FP8X4),
+                scales=scales[:, g - 1 : g + 1, :].rearrange("p g n -> p (g n)"),
+                in_=attn[u // 2][:].rearrange("p g n t -> p (g n t)"),
             )
 
-        def attn_times_values(b, c):
+        def quantise_part(u, a0, a1):
+            b, c, g = unit_indices(u)
+            codes, scales = packed_of(b, c)
+            queries = slice(a0 * P, a1 * P)
+            nc.vector.quantize_mx(
+                out=codes[:, g, queries].bitcast(FP8X4),
+                scales=scales[:, g, queries],
+                in_=attn_of(u)[:, queries, :].rearrange("p n t -> p (n t)"),
+            )
+
+        def attn_times_values(b, c, a, acc):
             codes, scales = packed[(b, c)]
-            acc = out_psum.tile([P, Q_TILES, DIM], F32)
-            for a in range(Q_TILES):
-                queries = slice(a * P, (a + 1) * P)
-                for g in range(GROUPS):
-                    nc.tensor.matmul_mx(
-                        out=acc[:, a, :],
-                        lhsT=codes[:, g, queries].bitcast(FP8X4),
-                        lhsT_scale=scales[:, g, queries],
-                        rhs=v_codes[:, b * GROUPS + g, :].bitcast(FP8X4),
-                        rhs_scale=v_scales[:, b * GROUPS + g, :],
-                        start=(g == 0),
-                        stop=(g == GROUPS - 1),
-                    )
-            sums[(b, c)] = acc
+            queries = slice(a * P, (a + 1) * P)
+            for g in range(GROUPS):
+                nc.tensor.matmul_mx(
+                    out=acc,
+                    lhsT=codes[:, g, queries].bitcast(FP8X4),
+                    lhsT_scale=scales[:, g, queries],
+                    rhs=v_codes[:, b, g, :].bitcast(FP8X4),
+                    rhs_scale=v_scales[:, b, g, :],
+                    start=(g == 0),
+                    stop=(g == GROUPS - 1),
+                )
 
-        def store(b, c):
-            result = result_pool.tile([P, Q_TILES, DIM], F32)
-            nc.scalar.copy(out=result[:], in_=sums[(b, c)][:])
+        def store(b, c, a0, a1, result):
+            tiles = slice(c * Q_TILES + a0, c * Q_TILES + a1)
             nc.sync.dma_start(
-                out=out[b, 0].rearrange("(j a) d -> j a d", a=ALL_Q_TILES)[:, c * Q_TILES : (c + 1) * Q_TILES, :],
-                in_=result[:],
+                out=out[b, 0].rearrange("(j a) d -> j a d", a=ALL_Q_TILES)[:, tiles, :],
+                in_=result,
             )
 
-        def is_unit(u):
-            return 0 <= u < UNITS
+        q1 = ("q", 0, 1)
+        blocks = [("q", 0, c) for c in range(2, CHUNKS)]
+        for b in range(1, BATCH):
+            blocks += [("q", b, 0)] + [("k", b, g) for g in range(GROUPS)]
+            blocks += [("q", b, c) for c in range(1, CHUNKS)]
+        tasks = [(flip, flip_out, q1), (fold_flip, fold_out, k3), (fold_flip, fold_out, q0)]
+        tasks += [(flip, flip_out, blocks[0]), (row, row_out, q1), (fold_flip, fold_out, q1), (flip, flip_out, blocks[1])]
+        for n, block in enumerate(blocks):
+            if n + 2 < len(blocks):
+                tasks.append((flip, flip_out, blocks[n + 2]))
+            tasks.append((norm, norm_out, block))
+            if n > 0 and blocks[n - 1][0] == "q":
+                tasks.append((row, row_out, blocks[n - 1]))
+            if n > 0 and (blocks[n - 1][0] == "q" or blocks[n - 1][2] == FOLD_GROUP):
+                tasks.append((fold_flip, fold_out, blocks[n - 1]))
+        tasks += [(row, row_out, blocks[-1]), (fold_flip, fold_out, blocks[-1])]
 
-        for step in range(-FLIP_AHEAD, UNITS + STORE_BEHIND + 1):
-            if is_unit(step + FLIP_AHEAD):
-                b, c, g = unit_indices(step + FLIP_AHEAD)
-                if g == 0:
-                    q_squares[(b, c)] = flip(q_raw[:, b, c, :, :], q_flipped[:, b, c, :])
-                if c == 0:
-                    k_squares[(b, g)] = flip(k_raw[:, b, g, :, :], k_flipped[:, b, g, :])
-            if is_unit(step):
-                scores_to_logits(step)
-            if is_unit(step + NORMS_AHEAD):
-                b, c, g = unit_indices(step + NORMS_AHEAD)
-                if g == 0:
-                    query_norms(b, c)
-                if c == 0:
-                    key_norms(b, g)
-            behind = step - VALUES_BEHIND
-            if is_unit(behind) and unit_indices(behind)[2] == GROUPS - 1:
-                attn_times_values(unit_indices(behind)[0], unit_indices(behind)[1])
-            behind = step - STORE_BEHIND
-            if is_unit(behind) and unit_indices(behind)[2] == GROUPS - 1:
-                store(unit_indices(behind)[0], unit_indices(behind)[1])
-            if is_unit(step - QUANTISE_BEHIND):
-                quantise(step - QUANTISE_BEHIND)
-            if is_unit(step):
-                exponentials(step)
+        def prepare():
+            if tasks:
+                start, finish, block = tasks.pop(0)
+                start(block)
+                finish(block)
+                if start is flip and block in blocks:
+                    square(block)
+                if start is norm and (block[0] == "q" or block[2] == FOLD_GROUP):
+                    split(block)
+
+        query_bias_by_vector(q0)
+        squares_by_scalar(k0)
+        flip(q0)
+        flip(k0)
+        flip_out(q0, nc.vector.tensor_copy)
+        flip_out(k0, nc.vector.tensor_copy)
+        bias_from_squares(k0)
+        row(q0)
+        row_out(q0)
+        squares_by_scalar(k1)
+        flip(k1)
+        flip_out(k1, nc.vector.tensor_copy)
+        split(q0)
+        group_values(0)
+
+        for u in range(UNITS):
+            b, c, g = unit_indices(u)
+            last = u == UNITS - 1
+            for t in range(PACK):
+                scores_to_logits(u, t)
+                if u > 0 and t % 2 == 1:
+                    prepare()
+                if u == 0 and t == 1:
+                    squares_by_scalar(k2)
+                    flip(k2)
+                    flip_out(k2, nc.vector.tensor_copy)
+                    bias_from_squares(k1)
+                if u == 1 and t == 0:
+                    bias_from_squares(k3)
+                    split(k3)
+                    bias_from_squares(q1)
+                    split(q1)
+                if u == 0 and t == 3:
+                    squares_by_scalar(k3)
+                    squares_by_scalar(q1)
+                    flip(k3)
+                    flip_out(k3, nc.vector.tensor_copy)
+                    bias_from_squares(k2)
+            if u == 1:
+                quantise_values(0)
+            if u == GROUPS:
+                group_values(1)
+            if u == 2 * GROUPS:
+                quantise_values(1)
+            if u % 2 == 1 and u > 1:
+                quantise_pair(u - 2)
+            done = u // GROUPS - 1
+            if done >= 0 and g == 2:
+                sums[done] = out_psum.tile([P, Q_TILES, DIM], F32, name="acc")
+                for a in range(Q_TILES):
+                    attn_times_values(done // CHUNKS, done % CHUNKS, a, sums[done][:, a, :])
+            if done >= 0 and g == 3:
+                result = result_pool.tile([P, Q_TILES, DIM], F32)
+                (nc.vector.tensor_copy if last else nc.scalar.copy)(out=result[:], in_=sums[done][:])
+                store(done // CHUNKS, done % CHUNKS, 0, Q_TILES, result[:])
+            if g == FOLD_GROUP:
+                for a in range(Q_TILES - folded_tiles(b, c), Q_TILES):
+                    folded_tile(u, a)
+            if not last:
+                exponentials(u, 0, subtracted_queries(u))
+
+        u = UNITS - 1
+        b, c, g = unit_indices(u)
+        quantise_part(u - 1, 0, Q_TILES)
+        folded_from = Q_TILES - folded_tiles(b, c)
+        quantise_part(u, folded_from, Q_TILES)
+        for a in range(folded_from):
+            exponentials(u, a * P, (a + 1) * P)
+            quantise_part(u, a, a + 1)
+        for a in list(range(folded_from, Q_TILES)) + list(range(folded_from)):
+            acc = score_psum.tile([P, DIM], F32, tag="scores")
+            attn_times_values(b, c, a, acc[:])
+            result = result_pool.tile([P, DIM], F32, name="last_result")
+            nc.vector.tensor_copy(out=result[:], in_=acc[:])
+            store(b, c, a, a + 1, result[:].rearrange("p (a d) -> p a d", a=1))

@@ -27,6 +27,7 @@ MASK_BIAS = 1.0e9
 RUN = 4
 
 FOLD_GROUP = GROUPS - 1
+FOLD_SLOT = 3
 PARTS = 3
 
 FLOPS = 2 * (2 * BATCH * TOKENS * TOKENS * DIM)
@@ -36,8 +37,8 @@ def unit_indices(u):
     return u // (CHUNKS * GROUPS), (u // GROUPS) % CHUNKS, u % GROUPS
 
 
-def folded_tiles(b, c):
-    return 2 - c % 2
+def is_folded(b, c, g):
+    return b == BATCH - 1 and c < CHUNKS - 1 and g == FOLD_GROUP
 
 
 def tile_softmaxattention_kde_pa_kernel(tc, q_s, k_s, v_s, mask, out):
@@ -51,8 +52,8 @@ def tile_softmaxattention_kde_pa_kernel(tc, q_s, k_s, v_s, mask, out):
         attn_pool = ctx.enter_context(tc.tile_pool(name="attn", bufs=3))
         packed_pool = ctx.enter_context(tc.tile_pool(name="packed", bufs=2))
         result_pool = ctx.enter_context(tc.tile_pool(name="result", bufs=4))
-        score_psum = ctx.enter_context(tc.psum_pool(name="score_psum", bufs=5))
-        prep_psum = ctx.enter_context(tc.psum_pool(name="prep_psum", bufs=2))
+        score_psum = ctx.enter_context(tc.psum_pool(name="score_psum", bufs=4))
+        prep_psum = ctx.enter_context(tc.psum_pool(name="prep_psum", bufs=3))
         out_psum = ctx.enter_context(tc.psum_pool(name="out_psum", bufs=1))
         ctx.enter_context(tc.manual_schedule())
 
@@ -62,10 +63,10 @@ def tile_softmaxattention_kde_pa_kernel(tc, q_s, k_s, v_s, mask, out):
         k_flipped = keep.tile([P, BATCH, GROUPS, GROUP], BF16)
         q_square = keep.tile([P, BATCH, CHUNKS, Q_TILES], F32)
         k_square = keep.tile([P, BATCH, GROUPS, PACK], F32)
-        k_terms = keep.tile([P, BATCH, PACK, P], BF16)
-        q_terms = keep.tile([P, 2, Q_TILES, P], BF16)
-        k_folds = keep.tile([P, BATCH, PACK, P], BF16)
-        q_folds = keep.tile([P, BATCH, CHUNKS, Q_TILES, P], BF16)
+        k_terms = keep.tile([P, PACK, P], BF16)
+        q_terms = keep.tile([P, CHUNKS, Q_TILES, P], BF16)
+        k_folds = keep.tile([P, PACK, P], BF16)
+        q_folds = keep.tile([P, CHUNKS, Q_TILES, P], BF16)
         q_column = keep.tile([P, BATCH, CHUNKS, Q_TILES], F32)
         q_row = keep.tile([P, BATCH, CHUNKS, CHUNK], F32)
         k_column = keep.tile([P, BATCH, GROUPS, PACK], F32)
@@ -117,9 +118,10 @@ def tile_softmaxattention_kde_pa_kernel(tc, q_s, k_s, v_s, mask, out):
         )
 
         prep = {}
+        prep = {}
         for terms, first_one in ((k_terms, PARTS), (q_terms, 0)):
             nc.gpsimd.memset(terms[:], 0.0)
-            nc.gpsimd.memset(terms[:, :, :, first_one : first_one + PARTS], 1.0)
+            nc.gpsimd.memset(terms[:, :, first_one : first_one + PARTS], 1.0)
 
         squares = {}
         logits = {}
@@ -210,34 +212,36 @@ def tile_softmaxattention_kde_pa_kernel(tc, q_s, k_s, v_s, mask, out):
             else:
                 nc.vector.tensor_tensor(out=k_column[:, b, n, :], in0=columns, in1=mask_term[:, b, n, :], op=ALU.add)
 
+        def is_in_fold(block):
+            kind, b, n = block
+            return is_folded(b, n, FOLD_GROUP) if kind == "q" else is_folded(b, 0, n)
+
         def terms_of(block):
             kind, b, n = block
             if kind == "k":
-                return k_column[:, b, n, :], k_terms[:, b, :, 0:PARTS], k_terms[:, b, :, :], k_folds[:, b, :, :]
-            tiles = slice(Q_TILES - folded_tiles(b, n), Q_TILES)
-            return (
-                q_column[:, b, n, tiles],
-                q_terms[:, n % 2, tiles, PARTS : 2 * PARTS],
-                q_terms[:, n % 2, tiles, :],
-                q_folds[:, b, n, tiles, :],
-            )
+                return k_column[:, b, n, :], k_terms[:, :, 0:PARTS], k_terms[:], k_folds[:]
+            return q_column[:, b, n, :], q_terms[:, n, :, PARTS : 2 * PARTS], q_terms[:, n, :, :], q_folds[:, n, :, :]
+
+        def fill_terms():
+            for terms, first_one in ((k_terms[:], PARTS), (q_terms[:].rearrange("p c a j -> p (c a) j"), 0)):
+                nc.gpsimd.memset(terms, 0.0)
+                nc.gpsimd.memset(terms[:, :, first_one : first_one + PARTS], 1.0)
 
         def split(block):
             left, parts = terms_of(block)[:2]
             for part in range(PARTS):
                 nc.gpsimd.tensor_copy(out=parts[:, :, part], in_=left)
                 if part + 1 < PARTS:
-                    rest = rest_pool.tile([P, PACK], F32, name="rest")[:, 0 : left.shape[1]]
-                    nc.gpsimd.tensor_tensor(out=rest, in0=left, in1=parts[:, :, part], op=ALU.subtract)
-                    left = rest
+                    rest = rest_pool.tile([P, PACK], F32)
+                    nc.gpsimd.tensor_tensor(out=rest[:], in0=left, in1=parts[:, :, part], op=ALU.subtract)
+                    left = rest[:]
 
         def fold_flip(block):
             terms = terms_of(block)[2]
             turned = prep_psum.tile([P, PACK, P], BF16, tag="prep", name="turned_terms")
-            tiles = terms.shape[1]
-            for t in range(tiles):
+            for t in range(PACK):
                 nc.tensor.transpose(turned[:, t, :], terms[:, t, :], identity[:])
-            prep[("fold", block)] = turned[:, 0:tiles, :]
+            prep[("fold", block)] = turned[:]
 
         def fold_out(block):
             nc.scalar.copy(out=terms_of(block)[3], in_=prep[("fold", block)])
@@ -253,28 +257,23 @@ def tile_softmaxattention_kde_pa_kernel(tc, q_s, k_s, v_s, mask, out):
             kind, b, c = block
             nc.scalar.copy(out=q_row[:, b, c, :], in_=prep[("row", block)])
 
-        def subtracted_queries(u):
-            b, c, g = unit_indices(u)
-            return CHUNK - (folded_tiles(b, c) * P if g == FOLD_GROUP else 0)
-
         def scores_to_logits(u, t):
             b, c, g = unit_indices(u)
-            queries = subtracted_queries(u)
             if t == 0:
                 logits[u] = logits_pool.tile([P, PACK, CHUNK], F32, name="unit_logits")
             scores = score_psum.tile([P, CHUNK], F32, tag="scores")
             nc.tensor.matmul(
-                out=scores[:, 0:queries],
+                out=scores[:],
                 lhsT=k_flipped[:, b, g, t * P : (t + 1) * P],
-                rhs=q_flipped[:, b, c, 0:queries],
+                rhs=q_flipped[:, b, c, :],
                 start=True,
                 stop=True,
             )
             nc.vector.scalar_tensor_tensor(
-                out=logits[u][:, t, 0:queries],
-                in0=scores[:, 0:queries],
+                out=logits[u][:, t, :],
+                in0=scores[:],
                 scalar=k_column[:, b, g, t : t + 1],
-                in1=q_row[:, b, c, 0:queries],
+                in1=q_row[:, b, c, :],
                 op0=ALU.add,
                 op1=ALU.add,
             )
@@ -282,7 +281,7 @@ def tile_softmaxattention_kde_pa_kernel(tc, q_s, k_s, v_s, mask, out):
         def folded_tile(u, a):
             b, c, g = unit_indices(u)
             queries = slice(a * P, (a + 1) * P)
-            bank = score_psum.tile([P, PACK, P], F32, tag="scores", name="bank")
+            bank = prep_psum.tile([P, PACK, P], F32, tag="prep", name="bank")
             for t in range(PACK):
                 nc.tensor.matmul(
                     out=bank[:, t, :],
@@ -293,8 +292,8 @@ def tile_softmaxattention_kde_pa_kernel(tc, q_s, k_s, v_s, mask, out):
                 )
                 nc.tensor.matmul(
                     out=bank[:, t, :],
-                    lhsT=k_folds[:, b, t, :],
-                    rhs=q_folds[:, b, c, a, :],
+                    lhsT=k_folds[:, t, :],
+                    rhs=q_folds[:, c, a, :],
                     start=False,
                     stop=True,
                 )
@@ -309,8 +308,8 @@ def tile_softmaxattention_kde_pa_kernel(tc, q_s, k_s, v_s, mask, out):
                 attn[u // 2] = attn_pool.tile([P, 2, CHUNK, PACK], BF16, align_bytes=64, name="pair_attn")
             return attn[u // 2][:, u % 2, :, :]
 
-        def exponentials(u, start, stop):
-            queries = slice(start, stop)
+        def exponentials(u, a0=0, a1=Q_TILES):
+            queries = slice(a0 * P, a1 * P)
             nc.scalar.activation(
                 out=attn_of(u)[:, queries, :].rearrange("p (c i) t -> p c t i", i=RUN),
                 in_=logits[u][:, :, queries].rearrange("p t (c i) -> p c t i", i=RUN),
@@ -387,17 +386,17 @@ def tile_softmaxattention_kde_pa_kernel(tc, q_s, k_s, v_s, mask, out):
         for b in range(1, BATCH):
             blocks += [("q", b, 0)] + [("k", b, g) for g in range(GROUPS)]
             blocks += [("q", b, c) for c in range(1, CHUNKS)]
-        tasks = [(flip, flip_out, q1), (fold_flip, fold_out, k3), (fold_flip, fold_out, q0)]
-        tasks += [(flip, flip_out, blocks[0]), (row, row_out, q1), (fold_flip, fold_out, q1), (flip, flip_out, blocks[1])]
+        tasks = [(flip, flip_out, q1), (flip, flip_out, blocks[0]), (row, row_out, q1), (flip, flip_out, blocks[1])]
         for n, block in enumerate(blocks):
             if n + 2 < len(blocks):
                 tasks.append((flip, flip_out, blocks[n + 2]))
             tasks.append((norm, norm_out, block))
             if n > 0 and blocks[n - 1][0] == "q":
                 tasks.append((row, row_out, blocks[n - 1]))
-            if n > 0 and (blocks[n - 1][0] == "q" or blocks[n - 1][2] == FOLD_GROUP):
-                tasks.append((fold_flip, fold_out, blocks[n - 1]))
-        tasks += [(row, row_out, blocks[-1]), (fold_flip, fold_out, blocks[-1])]
+            if n > 1 and is_in_fold(blocks[n - 2]):
+                tasks.append((fold_flip, fold_out, blocks[n - 2]))
+        tasks.append((row, row_out, blocks[-1]))
+        tasks += [(fold_flip, fold_out, block) for block in blocks[-2:] if is_in_fold(block)]
 
         def prepare():
             if tasks:
@@ -406,7 +405,7 @@ def tile_softmaxattention_kde_pa_kernel(tc, q_s, k_s, v_s, mask, out):
                 finish(block)
                 if start is flip and block in blocks:
                     square(block)
-                if start is norm and (block[0] == "q" or block[2] == FOLD_GROUP):
+                if start is norm and is_in_fold(block):
                     split(block)
 
         query_bias_by_vector(q0)
@@ -421,14 +420,16 @@ def tile_softmaxattention_kde_pa_kernel(tc, q_s, k_s, v_s, mask, out):
         squares_by_scalar(k1)
         flip(k1)
         flip_out(k1, nc.vector.tensor_copy)
-        split(q0)
         group_values(0)
 
         for u in range(UNITS):
             b, c, g = unit_indices(u)
             last = u == UNITS - 1
             for t in range(PACK):
-                scores_to_logits(u, t)
+                if t == FOLD_SLOT and is_folded(b, c, FOLD_GROUP):
+                    folded_tile(u - g + FOLD_GROUP, g)
+                if not is_folded(b, c, g):
+                    scores_to_logits(u, t)
                 if u > 0 and t % 2 == 1:
                     prepare()
                 if u == 0 and t == 1:
@@ -438,9 +439,7 @@ def tile_softmaxattention_kde_pa_kernel(tc, q_s, k_s, v_s, mask, out):
                     bias_from_squares(k1)
                 if u == 1 and t == 0:
                     bias_from_squares(k3)
-                    split(k3)
                     bias_from_squares(q1)
-                    split(q1)
                 if u == 0 and t == 3:
                     squares_by_scalar(k3)
                     squares_by_scalar(q1)
@@ -449,6 +448,7 @@ def tile_softmaxattention_kde_pa_kernel(tc, q_s, k_s, v_s, mask, out):
                     bias_from_squares(k2)
             if u == 1:
                 quantise_values(0)
+                fill_terms()
             if u == GROUPS:
                 group_values(1)
             if u == 2 * GROUPS:
@@ -464,21 +464,16 @@ def tile_softmaxattention_kde_pa_kernel(tc, q_s, k_s, v_s, mask, out):
                 result = result_pool.tile([P, Q_TILES, DIM], F32)
                 (nc.vector.tensor_copy if last else nc.scalar.copy)(out=result[:], in_=sums[done][:])
                 store(done // CHUNKS, done % CHUNKS, 0, Q_TILES, result[:])
-            if g == FOLD_GROUP:
-                for a in range(Q_TILES - folded_tiles(b, c), Q_TILES):
-                    folded_tile(u, a)
-            if not last:
-                exponentials(u, 0, subtracted_queries(u))
+            if not last and not is_folded(b, c, g):
+                exponentials(u)
 
         u = UNITS - 1
         b, c, g = unit_indices(u)
         quantise_part(u - 1, 0, Q_TILES)
-        folded_from = Q_TILES - folded_tiles(b, c)
-        quantise_part(u, folded_from, Q_TILES)
-        for a in range(folded_from):
-            exponentials(u, a * P, (a + 1) * P)
+        for a in range(Q_TILES):
+            exponentials(u, a, a + 1)
             quantise_part(u, a, a + 1)
-        for a in list(range(folded_from, Q_TILES)) + list(range(folded_from)):
+        for a in range(Q_TILES):
             acc = score_psum.tile([P, DIM], F32, tag="scores")
             attn_times_values(b, c, a, acc[:])
             result = result_pool.tile([P, DIM], F32, name="last_result")

@@ -28,6 +28,8 @@ RUN = 4
 
 FOLD_GROUP = GROUPS - 1
 FOLD_SLOT = 3
+LAST_FOLD_SLOTS = ((0, 3), (1, 3), (2, 0), (2, 1))
+LAST_SUBTRACTED = UNITS - 2
 PARTS = 3
 
 FLOPS = 2 * (2 * BATCH * TOKENS * TOKENS * DIM)
@@ -37,8 +39,16 @@ def unit_indices(u):
     return u // (CHUNKS * GROUPS), (u // GROUPS) % CHUNKS, u % GROUPS
 
 
-def is_folded(b, c, g):
+def is_folded_by_parts(b, c, g):
     return b == BATCH - 1 and c < CHUNKS - 1 and g == FOLD_GROUP
+
+
+def is_folded_by_transposes(b, c, g):
+    return b == BATCH - 1 and c == CHUNKS - 1 and g == FOLD_GROUP
+
+
+def is_folded(b, c, g):
+    return is_folded_by_parts(b, c, g) or is_folded_by_transposes(b, c, g)
 
 
 def tile_softmaxattention_kde_pa_kernel(tc, q_s, k_s, v_s, mask, out):
@@ -46,6 +56,7 @@ def tile_softmaxattention_kde_pa_kernel(tc, q_s, k_s, v_s, mask, out):
     with ExitStack() as ctx:
         keep = ctx.enter_context(tc.tile_pool(name="keep", bufs=1))
         squares_pool = ctx.enter_context(tc.tile_pool(name="squares", bufs=4))
+        bias_pool = ctx.enter_context(tc.tile_pool(name="bias", bufs=4))
         rest_pool = ctx.enter_context(tc.tile_pool(name="rest", bufs=4))
         unused_pool = ctx.enter_context(tc.tile_pool(name="unused", bufs=4))
         logits_pool = ctx.enter_context(tc.tile_pool(name="logits", bufs=3))
@@ -69,6 +80,7 @@ def tile_softmaxattention_kde_pa_kernel(tc, q_s, k_s, v_s, mask, out):
         q_folds = keep.tile([P, CHUNKS, Q_TILES, P], BF16)
         q_column = keep.tile([P, BATCH, CHUNKS, Q_TILES], F32)
         q_row = keep.tile([P, BATCH, CHUNKS, CHUNK], F32)
+        k_row = keep.tile([P, PACK, P], F32)
         k_column = keep.tile([P, BATCH, GROUPS, PACK], F32)
         mask_sb = keep.tile([P, BATCH * GROUPS, PACK], BF16)
         mask_term = keep.tile([P, BATCH, GROUPS, PACK], F32)
@@ -93,11 +105,12 @@ def tile_softmaxattention_kde_pa_kernel(tc, q_s, k_s, v_s, mask, out):
                 in_=k_s[b, 0, g * GROUP : (g + 1) * GROUP, :].rearrange("(p t) d -> p t d", t=PACK),
             )
 
-        nc.scalar.dma_start(out=mask_sb[:], in_=mask.rearrange("b (g p t) -> p (b g) t", p=P, t=PACK))
         for b in range(BATCH):
             load_queries(b, 0)
             for g in range(GROUPS):
                 load_keys(b, g)
+                if (b, g) == (0, 0):
+                    nc.sync.dma_start(out=mask_sb[:], in_=mask.rearrange("b (g p t) -> p (b g) t", p=P, t=PACK))
             load_queries(b, 1)
             nc.sync.dma_start(out=v_sb[:, b, :, :, :], in_=v_s[b, 0].rearrange("(g p t) d -> p g t d", p=P, t=PACK))
             for c in range(2, CHUNKS):
@@ -124,6 +137,7 @@ def tile_softmaxattention_kde_pa_kernel(tc, q_s, k_s, v_s, mask, out):
             nc.gpsimd.memset(terms[:, :, first_one : first_one + PARTS], 1.0)
 
         squares = {}
+        biases = {}
         logits = {}
         attn = {}
         packed = {}
@@ -150,7 +164,10 @@ def tile_softmaxattention_kde_pa_kernel(tc, q_s, k_s, v_s, mask, out):
 
         def square(block):
             squared = squares_pool.tile([P, PACK * P], F32)
-            nc.gpsimd.tensor_tensor(out=squared[:], in0=flipped(block), in1=flipped(block), op=ALU.mult)
+            for part in (slice(0, CHUNK // 2), slice(CHUNK // 2, CHUNK)):
+                nc.gpsimd.tensor_tensor(
+                    out=squared[:, part], in0=flipped(block)[:, part], in1=flipped(block)[:, part], op=ALU.mult
+                )
             squares[block] = squared
 
         def query_bias_by_vector(block):
@@ -214,7 +231,7 @@ def tile_softmaxattention_kde_pa_kernel(tc, q_s, k_s, v_s, mask, out):
 
         def is_in_fold(block):
             kind, b, n = block
-            return is_folded(b, n, FOLD_GROUP) if kind == "q" else is_folded(b, 0, n)
+            return is_folded_by_parts(b, n, FOLD_GROUP) if kind == "q" else is_folded_by_parts(b, 0, n)
 
         def terms_of(block):
             kind, b, n = block
@@ -247,38 +264,76 @@ def tile_softmaxattention_kde_pa_kernel(tc, q_s, k_s, v_s, mask, out):
             nc.scalar.copy(out=terms_of(block)[3], in_=prep[("fold", block)])
 
         def row(block):
-            kind, b, c = block
+            kind, b, n = block
+            column = q_column if kind == "q" else k_column
             rows = (score_psum if block == q0 else prep_psum).tile([P, Q_TILES, P], F32, tag="scores" if block == q0 else "prep", name="rows")
             for a in range(Q_TILES):
-                nc.tensor.transpose(rows[:, a, :], q_column[:, b, c, a : a + 1].to_broadcast([P, P]), identity_f32[:])
+                nc.tensor.transpose(rows[:, a, :], column[:, b, n, a : a + 1].to_broadcast([P, P]), identity_f32[:])
             prep[("row", block)] = rows[:].rearrange("p a n -> p (a n)")
 
         def row_out(block):
-            kind, b, c = block
-            nc.scalar.copy(out=q_row[:, b, c, :], in_=prep[("row", block)])
+            kind, b, n = block
+            target = q_row[:, b, n, :] if kind == "q" else k_row[:].rearrange("p t m -> p (t m)")
+            nc.scalar.copy(out=target, in_=prep[("row", block)])
 
-        def scores_to_logits(u, t):
+        def scores_to_logits(u, t, start, stop):
             b, c, g = unit_indices(u)
-            if t == 0:
+            if u not in logits:
                 logits[u] = logits_pool.tile([P, PACK, CHUNK], F32, name="unit_logits")
             scores = score_psum.tile([P, CHUNK], F32, tag="scores")
             nc.tensor.matmul(
-                out=scores[:],
+                out=scores[:, 0 : stop - start],
                 lhsT=k_flipped[:, b, g, t * P : (t + 1) * P],
-                rhs=q_flipped[:, b, c, :],
+                rhs=q_flipped[:, b, c, start:stop],
                 start=True,
                 stop=True,
             )
             nc.vector.scalar_tensor_tensor(
-                out=logits[u][:, t, :],
-                in0=scores[:],
+                out=logits[u][:, t, start:stop],
+                in0=scores[:, 0 : stop - start],
                 scalar=k_column[:, b, g, t : t + 1],
-                in1=q_row[:, b, c, :],
+                in1=q_row[:, b, c, start:stop],
                 op0=ALU.add,
                 op1=ALU.add,
             )
 
-        def folded_tile(u, a):
+        def make_biases(u, a):
+            b, c, g = unit_indices(u)
+            tile_biases = bias_pool.tile([P, PACK, P], F32)
+            nc.gpsimd.tensor_scalar(
+                out=tile_biases[:],
+                in0=k_row[:],
+                scalar1=q_column[:, b, c, a : a + 1],
+                scalar2=1.0,
+                op0=ALU.add,
+                op1=ALU.mult,
+            )
+            biases[(u, a)] = tile_biases
+
+        def folded_tile_by_transposes(u, a):
+            b, c, g = unit_indices(u)
+            queries = slice(a * P, (a + 1) * P)
+            bank = prep_psum.tile([P, PACK, P], F32, tag="prep", name="bank")
+            for t in range(PACK):
+                nc.tensor.matmul(
+                    out=bank[:, t, :],
+                    lhsT=biases[(u, a)][:, t, :],
+                    rhs=identity_f32[:],
+                    is_transpose=True,
+                    start=(t == 0),
+                    stop=False,
+                )
+            for t in range(PACK):
+                nc.tensor.matmul(
+                    out=bank[:, t, :],
+                    lhsT=k_flipped[:, b, g, t * P : (t + 1) * P],
+                    rhs=q_flipped[:, b, c, queries],
+                    start=False,
+                    stop=(t == PACK - 1),
+                )
+            folded_exp(u, a, bank)
+
+        def folded_tile_by_parts(u, a):
             b, c, g = unit_indices(u)
             queries = slice(a * P, (a + 1) * P)
             bank = prep_psum.tile([P, PACK, P], F32, tag="prep", name="bank")
@@ -297,8 +352,11 @@ def tile_softmaxattention_kde_pa_kernel(tc, q_s, k_s, v_s, mask, out):
                     start=False,
                     stop=True,
                 )
+            folded_exp(u, a, bank)
+
+        def folded_exp(u, a, bank):
             nc.scalar.activation(
-                out=attn_of(u)[:, queries, :],
+                out=attn_of(u)[:, a * P : (a + 1) * P, :],
                 in_=bank[:].rearrange("p t n -> p n t"),
                 func=ACT.Exp,
             )
@@ -397,6 +455,7 @@ def tile_softmaxattention_kde_pa_kernel(tc, q_s, k_s, v_s, mask, out):
                 tasks.append((fold_flip, fold_out, blocks[n - 2]))
         tasks.append((row, row_out, blocks[-1]))
         tasks += [(fold_flip, fold_out, block) for block in blocks[-2:] if is_in_fold(block)]
+        tasks.append((row, row_out, ("k", BATCH - 1, FOLD_GROUP)))
 
         def prepare():
             if tasks:
@@ -426,10 +485,17 @@ def tile_softmaxattention_kde_pa_kernel(tc, q_s, k_s, v_s, mask, out):
             b, c, g = unit_indices(u)
             last = u == UNITS - 1
             for t in range(PACK):
-                if t == FOLD_SLOT and is_folded(b, c, FOLD_GROUP):
-                    folded_tile(u - g + FOLD_GROUP, g)
-                if not is_folded(b, c, g):
-                    scores_to_logits(u, t)
+                if t == FOLD_SLOT and is_folded_by_parts(b, c, FOLD_GROUP):
+                    folded_tile_by_parts(u - g + FOLD_GROUP, g)
+                if is_folded_by_transposes(b, c, FOLD_GROUP) and (g, t) in LAST_FOLD_SLOTS:
+                    folded_tile_by_transposes(UNITS - 1, LAST_FOLD_SLOTS.index((g, t)))
+                if u == UNITS - GROUPS - 1:
+                    make_biases(UNITS - 1, t)
+                if u == LAST_SUBTRACTED:
+                    for t2 in (2 * t % PACK, 2 * t % PACK + 1):
+                        scores_to_logits(u, t2, t // 2 * (CHUNK // 2), (t // 2 + 1) * (CHUNK // 2))
+                elif not is_folded(b, c, g):
+                    scores_to_logits(u, t, 0, CHUNK)
                 if u > 0 and t % 2 == 1:
                     prepare()
                 if u == 0 and t == 1:
@@ -447,8 +513,9 @@ def tile_softmaxattention_kde_pa_kernel(tc, q_s, k_s, v_s, mask, out):
                     flip_out(k3, nc.vector.tensor_copy)
                     bias_from_squares(k2)
             if u == 1:
-                quantise_values(0)
                 fill_terms()
+            if u == 3:
+                quantise_values(0)
             if u == GROUPS:
                 group_values(1)
             if u == 2 * GROUPS:
@@ -464,15 +531,14 @@ def tile_softmaxattention_kde_pa_kernel(tc, q_s, k_s, v_s, mask, out):
                 result = result_pool.tile([P, Q_TILES, DIM], F32)
                 (nc.vector.tensor_copy if last else nc.scalar.copy)(out=result[:], in_=sums[done][:])
                 store(done // CHUNKS, done % CHUNKS, 0, Q_TILES, result[:])
-            if not last and not is_folded(b, c, g):
+            if u != LAST_SUBTRACTED and not is_folded(b, c, g):
                 exponentials(u)
 
-        u = UNITS - 1
-        b, c, g = unit_indices(u)
-        quantise_part(u - 1, 0, Q_TILES)
+        b, c, g = unit_indices(LAST_SUBTRACTED)
+        quantise_part(UNITS - 1, 0, Q_TILES)
         for a in range(Q_TILES):
-            exponentials(u, a, a + 1)
-            quantise_part(u, a, a + 1)
+            exponentials(LAST_SUBTRACTED, a, a + 1)
+            quantise_part(LAST_SUBTRACTED, a, a + 1)
         for a in range(Q_TILES):
             acc = score_psum.tile([P, DIM], F32, tag="scores")
             attn_times_values(b, c, a, acc[:])

@@ -28,6 +28,7 @@ RUN = 4
 
 FOLD_GROUP = GROUPS - 1
 FOLD_SLOT = 3
+PREPARE_SLOT = 2
 LAST_FOLD_SLOTS = ((0, 3), (1, 3), (2, 0), (2, 1))
 LAST_SUBTRACTED = UNITS - 2
 PARTS = 3
@@ -55,7 +56,7 @@ def tile_softmaxattention_kde_pa_kernel(tc, q_s, k_s, v_s, mask, out):
     nc = tc.nc
     with ExitStack() as ctx:
         keep = ctx.enter_context(tc.tile_pool(name="keep", bufs=1))
-        squares_pool = ctx.enter_context(tc.tile_pool(name="squares", bufs=4))
+        tree_pool = ctx.enter_context(tc.tile_pool(name="tree", bufs=2))
         bias_pool = ctx.enter_context(tc.tile_pool(name="bias", bufs=4))
         rest_pool = ctx.enter_context(tc.tile_pool(name="rest", bufs=4))
         unused_pool = ctx.enter_context(tc.tile_pool(name="unused", bufs=4))
@@ -82,7 +83,7 @@ def tile_softmaxattention_kde_pa_kernel(tc, q_s, k_s, v_s, mask, out):
         q_row = keep.tile([P, BATCH, CHUNKS, CHUNK], F32)
         k_row = keep.tile([P, PACK, P], F32)
         k_column = keep.tile([P, BATCH, GROUPS, PACK], F32)
-        mask_sb = keep.tile([P, BATCH * GROUPS, PACK], BF16)
+        mask_sb = keep.tile([P, GROUP], BF16)
         mask_term = keep.tile([P, BATCH, GROUPS, PACK], F32)
         v_sb = keep.tile([P, BATCH, GROUPS, PACK, DIM], BF16)
         v_grouped = keep.tile([P, BATCH, GROUPS, DIM, PACK], BF16, align_bytes=64)
@@ -90,7 +91,6 @@ def tile_softmaxattention_kde_pa_kernel(tc, q_s, k_s, v_s, mask, out):
         v_scales = keep.tile([P, BATCH, GROUPS, DIM], U8, align_bytes=64)
         identity = keep.tile([P, P], BF16)
         identity_f32 = keep.tile([P, P], F32)
-        minus_half = keep.tile([P, 1], F32)
         warm = keep.tile([P, 1], F32)
 
         def load_queries(b, c):
@@ -105,12 +105,15 @@ def tile_softmaxattention_kde_pa_kernel(tc, q_s, k_s, v_s, mask, out):
                 in_=k_s[b, 0, g * GROUP : (g + 1) * GROUP, :].rearrange("(p t) d -> p t d", t=PACK),
             )
 
+        nc.gpsimd.memset(mask_sb[:].bitcast(U32), 0)
         for b in range(BATCH):
             load_queries(b, 0)
             for g in range(GROUPS):
                 load_keys(b, g)
                 if (b, g) == (0, 0):
-                    nc.sync.dma_start(out=mask_sb[:], in_=mask.rearrange("b (g p t) -> p (b g) t", p=P, t=PACK))
+                    nc.sync.dma_start(
+                        out=mask_sb[0 : BATCH * GROUPS, :], in_=mask.rearrange("b (g n) -> (b g) n", g=GROUPS)
+                    )
             load_queries(b, 1)
             nc.sync.dma_start(out=v_sb[:, b, :, :, :], in_=v_s[b, 0].rearrange("(g p t) d -> p g t d", p=P, t=PACK))
             for c in range(2, CHUNKS):
@@ -119,31 +122,20 @@ def tile_softmaxattention_kde_pa_kernel(tc, q_s, k_s, v_s, mask, out):
         make_identity(nc, identity[:])
         make_identity(nc, identity_f32[:])
         nc.vector.memset(warm[:], 0.0)
-        nc.vector.memset(minus_half[:], -0.5)
         nc.scalar.activation(out=warm[:], in_=warm[:], func=ACT.Exp)
-        nc.gpsimd.tensor_scalar(
-            out=mask_term[:].rearrange("p b g t -> p (b g) t"),
-            in0=mask_sb[:],
-            scalar1=MASK_BIAS,
-            scalar2=-MASK_BIAS,
-            op0=ALU.mult,
-            op1=ALU.add,
-        )
-
         prep = {}
         prep = {}
         for terms, first_one in ((k_terms, PARTS), (q_terms, 0)):
             nc.gpsimd.memset(terms[:], 0.0)
             nc.gpsimd.memset(terms[:, :, first_one : first_one + PARTS], 1.0)
 
-        squares = {}
         biases = {}
         logits = {}
         attn = {}
         packed = {}
         sums = {}
 
-        q0, k0, k1, k2, k3 = [("q", 0, 0)] + [("k", 0, g) for g in range(GROUPS)]
+        q0, q1, k0, k1, k2, k3 = [("q", 0, 0), ("q", 0, 1)] + [("k", 0, g) for g in range(GROUPS)]
 
         def raw(block):
             kind, b, n = block
@@ -159,16 +151,8 @@ def tile_softmaxattention_kde_pa_kernel(tc, q_s, k_s, v_s, mask, out):
                 nc.tensor.transpose(turned[:, a, :], raw(block)[:, a, :], identity[:])
             prep[("flip", block)] = turned[:].rearrange("p a j -> p (a j)")
 
-        def flip_out(block, engine_copy=nc.scalar.copy):
+        def flip_out(block, engine_copy):
             engine_copy(out=flipped(block), in_=prep[("flip", block)])
-
-        def square(block):
-            squared = squares_pool.tile([P, PACK * P], F32)
-            for part in (slice(0, CHUNK // 2), slice(CHUNK // 2, CHUNK)):
-                nc.gpsimd.tensor_tensor(
-                    out=squared[:, part], in0=flipped(block)[:, part], in1=flipped(block)[:, part], op=ALU.mult
-                )
-            squares[block] = squared
 
         def query_bias_by_vector(block):
             kind, b, n = block
@@ -209,25 +193,28 @@ def tile_softmaxattention_kde_pa_kernel(tc, q_s, k_s, v_s, mask, out):
                     op1=ALU.add,
                 )
 
-        def norm(block):
-            columns = prep_psum.tile([P, PACK], F32, tag="prep")
-            for t in range(PACK):
-                nc.tensor.matmul(
-                    out=columns[:, t : t + 1],
-                    lhsT=squares[block][:, t * P : (t + 1) * P],
-                    rhs=minus_half[:],
-                    start=True,
-                    stop=True,
-                )
-            prep[("norm", block)] = columns[:]
-
-        def norm_out(block):
+        def query_bias_by_gpsimd(block):
             kind, b, n = block
-            columns = prep[("norm", block)]
-            if kind == "q":
-                nc.scalar.copy(out=q_column[:, b, n, :], in_=columns)
-            else:
-                nc.vector.tensor_tensor(out=k_column[:, b, n, :], in0=columns, in1=mask_term[:, b, n, :], op=ALU.add)
+            tree = tree_pool.tile([P, Q_TILES, 2 * DIM], F32)
+            nc.gpsimd.tensor_tensor(out=tree[:, :, 0:DIM], in0=raw(block), in1=raw(block), op=ALU.mult)
+            start, width = 0, DIM
+            while width > 1:
+                half = width // 2
+                nc.gpsimd.tensor_tensor(
+                    out=tree[:, :, start + width : start + width + half],
+                    in0=tree[:, :, start : start + half],
+                    in1=tree[:, :, start + half : start + width],
+                    op=ALU.add,
+                )
+                start, width = start + width, half
+            nc.gpsimd.tensor_scalar(
+                out=q_column[:, b, n, :],
+                in0=tree[:, :, start],
+                scalar1=-0.5,
+                scalar2=0.0,
+                op0=ALU.mult,
+                op1=ALU.add,
+            )
 
         def is_in_fold(block):
             kind, b, n = block
@@ -260,8 +247,8 @@ def tile_softmaxattention_kde_pa_kernel(tc, q_s, k_s, v_s, mask, out):
                 nc.tensor.transpose(turned[:, t, :], terms[:, t, :], identity[:])
             prep[("fold", block)] = turned[:]
 
-        def fold_out(block):
-            nc.scalar.copy(out=terms_of(block)[3], in_=prep[("fold", block)])
+        def fold_out(block, engine_copy):
+            engine_copy(out=terms_of(block)[3], in_=prep[("fold", block)])
 
         def row(block):
             kind, b, n = block
@@ -271,10 +258,10 @@ def tile_softmaxattention_kde_pa_kernel(tc, q_s, k_s, v_s, mask, out):
                 nc.tensor.transpose(rows[:, a, :], column[:, b, n, a : a + 1].to_broadcast([P, P]), identity_f32[:])
             prep[("row", block)] = rows[:].rearrange("p a n -> p (a n)")
 
-        def row_out(block):
+        def row_out(block, engine_copy):
             kind, b, n = block
             target = q_row[:, b, n, :] if kind == "q" else k_row[:].rearrange("p t m -> p (t m)")
-            nc.scalar.copy(out=target, in_=prep[("row", block)])
+            engine_copy(out=target, in_=prep[("row", block)])
 
         def scores_to_logits(u, t, start, stop):
             b, c, g = unit_indices(u)
@@ -439,43 +426,64 @@ def tile_softmaxattention_kde_pa_kernel(tc, q_s, k_s, v_s, mask, out):
                 in_=result,
             )
 
-        q1 = ("q", 0, 1)
-        blocks = [("q", 0, c) for c in range(2, CHUNKS)]
-        for b in range(1, BATCH):
-            blocks += [("q", b, 0)] + [("k", b, g) for g in range(GROUPS)]
-            blocks += [("q", b, c) for c in range(1, CHUNKS)]
-        tasks = [(flip, flip_out, q1), (flip, flip_out, blocks[0]), (row, row_out, q1), (flip, flip_out, blocks[1])]
-        for n, block in enumerate(blocks):
-            if n + 2 < len(blocks):
-                tasks.append((flip, flip_out, blocks[n + 2]))
-            tasks.append((norm, norm_out, block))
-            if n > 0 and blocks[n - 1][0] == "q":
-                tasks.append((row, row_out, blocks[n - 1]))
-            if n > 1 and is_in_fold(blocks[n - 2]):
-                tasks.append((fold_flip, fold_out, blocks[n - 2]))
-        tasks.append((row, row_out, blocks[-1]))
-        tasks += [(fold_flip, fold_out, block) for block in blocks[-2:] if is_in_fold(block)]
-        tasks.append((row, row_out, ("k", BATCH - 1, FOLD_GROUP)))
+        def queries_of(chunk):
+            return ("q",) + divmod(chunk, CHUNKS)
 
-        def prepare():
-            if tasks:
-                start, finish, block = tasks.pop(0)
-                start(block)
-                finish(block)
-                if start is flip and block in blocks:
-                    square(block)
-                if start is norm and is_in_fold(block):
-                    split(block)
+        def prepare(start, finish, block, engine_copy=nc.scalar.copy):
+            start(block)
+            finish(block, engine_copy)
+
+        def prepare_ahead(b, c, g):
+            chunk = b * CHUNKS + c
+            group = ("k", b + 1, (c + FOLD_GROUP) % GROUPS) if b + 1 < BATCH else None
+            copy = nc.scalar.copy if b == 0 else nc.vector.tensor_copy
+            following = queries_of(chunk + 1) if chunk + 1 < BATCH * CHUNKS else None
+            if g == 0 and following:
+                prepare(flip, flip_out, following, copy)
+            if g == 0 and chunk + 2 < BATCH * CHUNKS:
+                query_bias_by_gpsimd(queries_of(chunk + 2))
+                if is_in_fold(queries_of(chunk + 2)):
+                    split(queries_of(chunk + 2))
+            if g == 1 and group:
+                prepare(flip, flip_out, group)
+            if g == 2 and following:
+                prepare(row, row_out, following)
+            if g == 2 and group:
+                squares_by_scalar(group)
+            if g == 3 and group:
+                bias_from_squares(group)
+                if is_in_fold(group):
+                    split(group)
+            if g == 3 and following and is_in_fold(following):
+                prepare(fold_flip, fold_out, following, copy)
+            if g == 3 and chunk == 1:
+                prepare(fold_flip, fold_out, ("k", 1, FOLD_GROUP))
+            if g == 1 and chunk == BATCH * CHUNKS - 2:
+                prepare(row, row_out, ("k", 1, FOLD_GROUP))
+
+        def spread_mask():
+            turned = score_psum.tile([P, PACK, P], BF16, tag="scores", name="turned_mask")
+            for t in range(PACK):
+                nc.tensor.transpose(turned[:, t, :], mask_sb[:, t:GROUP:PACK], identity[:])
+            nc.vector.tensor_scalar(
+                out=mask_term[:].rearrange("p b g t -> p (b g) t"),
+                in0=turned[:, :, 0 : BATCH * GROUPS].rearrange("p t g -> p g t"),
+                scalar1=MASK_BIAS,
+                scalar2=-MASK_BIAS,
+                op0=ALU.mult,
+                op1=ALU.add,
+            )
 
         query_bias_by_vector(q0)
         squares_by_scalar(k0)
         flip(q0)
         flip(k0)
         flip_out(q0, nc.vector.tensor_copy)
-        flip_out(k0, nc.vector.tensor_copy)
-        bias_from_squares(k0)
         row(q0)
-        row_out(q0)
+        row_out(q0, nc.scalar.copy)
+        flip_out(k0, nc.vector.tensor_copy)
+        spread_mask()
+        bias_from_squares(k0)
         squares_by_scalar(k1)
         flip(k1)
         flip_out(k1, nc.vector.tensor_copy)
@@ -496,8 +504,8 @@ def tile_softmaxattention_kde_pa_kernel(tc, q_s, k_s, v_s, mask, out):
                         scores_to_logits(u, t2, t // 2 * (CHUNK // 2), (t // 2 + 1) * (CHUNK // 2))
                 elif not is_folded(b, c, g):
                     scores_to_logits(u, t, 0, CHUNK)
-                if u > 0 and t % 2 == 1:
-                    prepare()
+                if t == PREPARE_SLOT:
+                    prepare_ahead(b, c, g)
                 if u == 0 and t == 1:
                     squares_by_scalar(k2)
                     flip(k2)
@@ -512,7 +520,7 @@ def tile_softmaxattention_kde_pa_kernel(tc, q_s, k_s, v_s, mask, out):
                     flip(k3)
                     flip_out(k3, nc.vector.tensor_copy)
                     bias_from_squares(k2)
-            if u == 1:
+            if u == 2:
                 fill_terms()
             if u == 3:
                 quantise_values(0)

@@ -29,6 +29,7 @@ RUN = 4
 FOLD_GROUP = GROUPS - 1
 FOLD_SLOT = 3
 PREPARE_SLOT = 2
+SUMMED_BY_SCALAR = 3
 LAST_FOLD_SLOTS = ((0, 3), (1, 3), (2, 0), (2, 1))
 LAST_SUBTRACTED = UNITS - 2
 PARTS = 3
@@ -92,6 +93,7 @@ def tile_softmaxattention_kde_pa_kernel(tc, q_s, k_s, v_s, mask, out):
         identity = keep.tile([P, P], BF16)
         identity_f32 = keep.tile([P, P], F32)
         warm = keep.tile([P, 1], F32)
+        seen = keep.tile([P, PACK], U8)
 
         def load_queries(b, c):
             nc.sync.dma_start(
@@ -129,6 +131,7 @@ def tile_softmaxattention_kde_pa_kernel(tc, q_s, k_s, v_s, mask, out):
             nc.gpsimd.memset(terms[:], 0.0)
             nc.gpsimd.memset(terms[:, :, first_one : first_one + PARTS], 1.0)
 
+        unit_of_last_quantise = [None, None]
         biases = {}
         logits = {}
         attn = {}
@@ -284,18 +287,19 @@ def tile_softmaxattention_kde_pa_kernel(tc, q_s, k_s, v_s, mask, out):
                 op1=ALU.add,
             )
 
-        def make_biases(u, a):
+        def make_biases(u):
             b, c, g = unit_indices(u)
-            tile_biases = bias_pool.tile([P, PACK, P], F32)
-            nc.gpsimd.tensor_scalar(
-                out=tile_biases[:],
-                in0=k_row[:],
-                scalar1=q_column[:, b, c, a : a + 1],
-                scalar2=1.0,
-                op0=ALU.add,
-                op1=ALU.mult,
-            )
-            biases[(u, a)] = tile_biases
+            for a in range(Q_TILES):
+                tile_biases = bias_pool.tile([P, PACK, P], F32)
+                nc.gpsimd.tensor_scalar(
+                    out=tile_biases[:],
+                    in0=k_row[:],
+                    scalar1=q_column[:, b, c, a : a + 1],
+                    scalar2=1.0,
+                    op0=ALU.add,
+                    op1=ALU.mult,
+                )
+                biases[(u, a)] = tile_biases
 
         def folded_tile_by_transposes(u, a):
             b, c, g = unit_indices(u)
@@ -394,6 +398,7 @@ def tile_softmaxattention_kde_pa_kernel(tc, q_s, k_s, v_s, mask, out):
                 scales=scales[:, g - 1 : g + 1, :].rearrange("p g n -> p (g n)"),
                 in_=attn[u // 2][:].rearrange("p g n t -> p (g n t)"),
             )
+            unit_of_last_quantise[:] = [(b, c), g]
 
         def quantise_part(u, a0, a1):
             b, c, g = unit_indices(u)
@@ -440,10 +445,10 @@ def tile_softmaxattention_kde_pa_kernel(tc, q_s, k_s, v_s, mask, out):
             following = queries_of(chunk + 1) if chunk + 1 < BATCH * CHUNKS else None
             if g == 0 and following:
                 prepare(flip, flip_out, following, copy)
-            if g == 0 and chunk + 2 < BATCH * CHUNKS:
-                query_bias_by_gpsimd(queries_of(chunk + 2))
-                if is_in_fold(queries_of(chunk + 2)):
-                    split(queries_of(chunk + 2))
+            if g == 0 and chunk < SUMMED_BY_SCALAR:
+                squares_by_scalar(queries_of(chunk + 2))
+            if g == 1 and chunk < SUMMED_BY_SCALAR:
+                bias_from_squares(queries_of(chunk + 2))
             if g == 1 and group:
                 prepare(flip, flip_out, group)
             if g == 2 and following:
@@ -452,14 +457,31 @@ def tile_softmaxattention_kde_pa_kernel(tc, q_s, k_s, v_s, mask, out):
                 squares_by_scalar(group)
             if g == 3 and group:
                 bias_from_squares(group)
-                if is_in_fold(group):
-                    split(group)
             if g == 3 and following and is_in_fold(following):
                 prepare(fold_flip, fold_out, following, copy)
             if g == 3 and chunk == 1:
                 prepare(fold_flip, fold_out, ("k", 1, FOLD_GROUP))
             if g == 1 and chunk == BATCH * CHUNKS - 2:
                 prepare(row, row_out, ("k", 1, FOLD_GROUP))
+
+        def gpsimd_work(chunk, g):
+            b, c = divmod(chunk, CHUNKS)
+            work = []
+            if g == 1 and SUMMED_BY_SCALAR <= chunk < BATCH * CHUNKS - 2:
+                work.append((query_bias_by_gpsimd, queries_of(chunk + 2)))
+            if g == 1 and chunk < BATCH * CHUNKS - 2 and is_in_fold(queries_of(chunk + 2)):
+                work.append((split, queries_of(chunk + 2)))
+            if g == 3 and chunk == 0:
+                work.append((group_values, 1))
+            if g == 1 and chunk == 1:
+                work.append((split, ("k", 1, FOLD_GROUP)))
+            if g == 1 and chunk == BATCH * CHUNKS - 2:
+                work.append((make_biases, UNITS - 1))
+            if work:
+                scales = packed[unit_of_last_quantise[0]][1]
+                nc.gpsimd.tensor_copy(out=seen[:], in_=scales[:, unit_of_last_quantise[1], 0:PACK])
+            for task, argument in work:
+                task(argument)
 
         def spread_mask():
             turned = score_psum.tile([P, PACK, P], BF16, tag="scores", name="turned_mask")
@@ -487,6 +509,7 @@ def tile_softmaxattention_kde_pa_kernel(tc, q_s, k_s, v_s, mask, out):
         squares_by_scalar(k1)
         flip(k1)
         flip_out(k1, nc.vector.tensor_copy)
+        fill_terms()
         group_values(0)
 
         for u in range(UNITS):
@@ -497,8 +520,6 @@ def tile_softmaxattention_kde_pa_kernel(tc, q_s, k_s, v_s, mask, out):
                     folded_tile_by_parts(u - g + FOLD_GROUP, g)
                 if is_folded_by_transposes(b, c, FOLD_GROUP) and (g, t) in LAST_FOLD_SLOTS:
                     folded_tile_by_transposes(UNITS - 1, LAST_FOLD_SLOTS.index((g, t)))
-                if u == UNITS - GROUPS - 1:
-                    make_biases(UNITS - 1, t)
                 if u == LAST_SUBTRACTED:
                     for t2 in (2 * t % PACK, 2 * t % PACK + 1):
                         scores_to_logits(u, t2, t // 2 * (CHUNK // 2), (t // 2 + 1) * (CHUNK // 2))
@@ -520,16 +541,13 @@ def tile_softmaxattention_kde_pa_kernel(tc, q_s, k_s, v_s, mask, out):
                     flip(k3)
                     flip_out(k3, nc.vector.tensor_copy)
                     bias_from_squares(k2)
-            if u == 2:
-                fill_terms()
             if u == 3:
                 quantise_values(0)
-            if u == GROUPS:
-                group_values(1)
             if u == 2 * GROUPS:
                 quantise_values(1)
             if u % 2 == 1 and u > 1:
                 quantise_pair(u - 2)
+                gpsimd_work(b * CHUNKS + c, g)
             done = u // GROUPS - 1
             if done >= 0 and g == 2:
                 sums[done] = out_psum.tile([P, Q_TILES, DIM], F32, name="acc")

@@ -61,8 +61,8 @@ def tile_softmaxattention_kde_pa_kernel(tc, q_s, k_s, v_s, mask, out):
         bias_pool = ctx.enter_context(tc.tile_pool(name="bias", bufs=4))
         rest_pool = ctx.enter_context(tc.tile_pool(name="rest", bufs=4))
         unused_pool = ctx.enter_context(tc.tile_pool(name="unused", bufs=4))
-        logits_pool = ctx.enter_context(tc.tile_pool(name="logits", bufs=3))
-        attn_pool = ctx.enter_context(tc.tile_pool(name="attn", bufs=3))
+        logits_pool = ctx.enter_context(tc.tile_pool(name="logits", bufs=4))
+        attn_pool = ctx.enter_context(tc.tile_pool(name="attn", bufs=4))
         packed_pool = ctx.enter_context(tc.tile_pool(name="packed", bufs=2))
         result_pool = ctx.enter_context(tc.tile_pool(name="result", bufs=4))
         score_psum = ctx.enter_context(tc.psum_pool(name="score_psum", bufs=4))
@@ -126,10 +126,6 @@ def tile_softmaxattention_kde_pa_kernel(tc, q_s, k_s, v_s, mask, out):
         nc.vector.memset(warm[:], 0.0)
         nc.scalar.activation(out=warm[:], in_=warm[:], func=ACT.Exp)
         prep = {}
-        prep = {}
-        for terms, first_one in ((k_terms, PARTS), (q_terms, 0)):
-            nc.gpsimd.memset(terms[:], 0.0)
-            nc.gpsimd.memset(terms[:, :, first_one : first_one + PARTS], 1.0)
 
         unit_of_last_quantise = [None, None]
         biases = {}

@@ -24,13 +24,30 @@ Q_TILES = CHUNK // P
 ALL_Q_TILES = TOKENS // P
 UNITS = BATCH * CHUNKS * GROUPS
 MASK_BIAS = 1.0e9
+ROOT_HALF = 0.5**0.5
 RUN = 4
 
 FOLD_GROUP = GROUPS - 1
 FOLD_SLOT = 3
-PREPARE_SLOT = 2
-SUMMED_BY_SCALAR = 3
+TRANSPOSED = ((), (3,), (3,), (3,), (), (), (), (3,))
+TURNS = {0: ((0, (1, 2), (1, 3), (("k", 0, 3), ("q", 0, 1))), (0, (3, 2), (3, 3), (("q", 0, 2),))), 1: ((0, (2, 2), (2, 3), (("q", 0, 3),)),), 2: ((1, (2, 2), (2, 3), (("q", 1, 0),)),), 3: ((1, (2, 2), (2, 3), (("q", 1, 1),)),), 4: ((1, (2, 2), (2, 3), (("q", 1, 2), ("k", 1, 3))),), 5: ((1, (2, 2), (2, 3), (("q", 1, 3),)),)}
+FILL_AT = (2, 3)
+VALUES_AT = 5
+FIRST_QUANT = 4
+FLIP_Q_BY = "vvvvvvvv"
+FLIP_K_BY = "vvvvvvvv"
+SQUARE_Q_BY = "ssssssss"
+SQUARE_K_BY = "ssssssss"
+FOLD_BY = "vvvvvvvv"
+RESULT_BY = "ssssssss"
+FLIP_Q = ((1, 1), (0, 3))
+FLIP_K = ((1, 3), (1, 3))
+SQUARE_Q = ((0, 2), (1, 1))
+SQUARE_K = ((2, 2), (3, 1))
+FOLD_Q = ((3, 1), (3, 3))
 LAST_FOLD_SLOTS = ((0, 3), (1, 3), (2, 0), (2, 1))
+FOLD_SLOTS = ((0, 3), (1, 3), (2, 3), (3, 3))
+FOLD_SLOTS2 = ((0, 1), (0, 3), (1, 1), (1, 3), (2, 1), (2, 3), (3, 1), (3, 3))
 LAST_SUBTRACTED = UNITS - 2
 PARTS = 3
 
@@ -46,7 +63,7 @@ def is_folded_by_parts(b, c, g):
 
 
 def is_folded_by_transposes(b, c, g):
-    return b == BATCH - 1 and c == CHUNKS - 1 and g == FOLD_GROUP
+    return g in TRANSPOSED[b * CHUNKS + c]
 
 
 def is_folded(b, c, g):
@@ -57,8 +74,7 @@ def tile_softmaxattention_kde_pa_kernel(tc, q_s, k_s, v_s, mask, out):
     nc = tc.nc
     with ExitStack() as ctx:
         keep = ctx.enter_context(tc.tile_pool(name="keep", bufs=1))
-        tree_pool = ctx.enter_context(tc.tile_pool(name="tree", bufs=2))
-        bias_pool = ctx.enter_context(tc.tile_pool(name="bias", bufs=4))
+        bias_pool = ctx.enter_context(tc.tile_pool(name="bias", bufs=16))
         rest_pool = ctx.enter_context(tc.tile_pool(name="rest", bufs=4))
         unused_pool = ctx.enter_context(tc.tile_pool(name="unused", bufs=4))
         logits_pool = ctx.enter_context(tc.tile_pool(name="logits", bufs=4))
@@ -74,16 +90,17 @@ def tile_softmaxattention_kde_pa_kernel(tc, q_s, k_s, v_s, mask, out):
         k_raw = keep.tile([P, BATCH, GROUPS, PACK, DIM], BF16)
         q_flipped = keep.tile([P, BATCH, CHUNKS, CHUNK], BF16)
         k_flipped = keep.tile([P, BATCH, GROUPS, GROUP], BF16)
-        q_square = keep.tile([P, BATCH, CHUNKS, Q_TILES], F32)
         k_square = keep.tile([P, BATCH, GROUPS, PACK], F32)
         k_terms = keep.tile([P, PACK, P], BF16)
         q_terms = keep.tile([P, CHUNKS, Q_TILES, P], BF16)
         k_folds = keep.tile([P, PACK, P], BF16)
         q_folds = keep.tile([P, CHUNKS, Q_TILES, P], BF16)
-        q_column = keep.tile([P, BATCH, CHUNKS, Q_TILES], F32)
+        columns = keep.tile([P, BATCH, P], F32)
+        row_parts = keep.tile([4 * CHUNKS + 4 * GROUPS, 4, P], F32)
+        q_column = columns[:, :, 0 : CHUNKS * Q_TILES].rearrange("p b (c a) -> p b c a", a=Q_TILES)
+        k_column = columns[:, :, CHUNKS * Q_TILES : CHUNKS * Q_TILES + GROUPS * PACK].rearrange("p b (g t) -> p b g t", t=PACK)
         q_row = keep.tile([P, BATCH, CHUNKS, CHUNK], F32)
-        k_row = keep.tile([P, PACK, P], F32)
-        k_column = keep.tile([P, BATCH, GROUPS, PACK], F32)
+        k_row = keep.tile([P, BATCH, GROUPS, PACK, P], F32)
         mask_sb = keep.tile([P, GROUP], BF16)
         mask_term = keep.tile([P, BATCH, GROUPS, PACK], F32)
         v_sb = keep.tile([P, BATCH, GROUPS, PACK, DIM], BF16)
@@ -95,31 +112,38 @@ def tile_softmaxattention_kde_pa_kernel(tc, q_s, k_s, v_s, mask, out):
         warm = keep.tile([P, 1], F32)
         seen = keep.tile([P, PACK], U8)
 
-        def load_queries(b, c):
+        def load_queries(b, c0, c1):
             nc.sync.dma_start(
-                out=q_raw[:, b, c, :, :],
-                in_=q_s[b, 0].rearrange("(j a) d -> j a d", a=ALL_Q_TILES)[:, c * Q_TILES : (c + 1) * Q_TILES, :],
+                out=q_raw[:, b, c0:c1, :, :],
+                in_=q_s[b, 0].rearrange("(j c a) d -> j c a d", c=CHUNKS, a=Q_TILES)[:, c0:c1, :, :],
             )
 
-        def load_keys(b, g):
+        def load_keys(b, g0, g1):
             nc.sync.dma_start(
-                out=k_raw[:, b, g, :, :],
-                in_=k_s[b, 0, g * GROUP : (g + 1) * GROUP, :].rearrange("(p t) d -> p t d", t=PACK),
+                out=k_raw[:, b, g0:g1, :, :],
+                in_=k_s[b, 0].rearrange("(g p t) d -> p g t d", p=P, t=PACK)[:, g0:g1, :, :],
             )
+
+        def load_values(b):
+            nc.sync.dma_start(out=v_sb[:, b, :, :, :], in_=v_s[b, 0].rearrange("(g p t) d -> p g t d", p=P, t=PACK))
 
         nc.gpsimd.memset(mask_sb[:].bitcast(U32), 0)
-        for b in range(BATCH):
-            load_queries(b, 0)
-            for g in range(GROUPS):
-                load_keys(b, g)
-                if (b, g) == (0, 0):
-                    nc.sync.dma_start(
-                        out=mask_sb[0 : BATCH * GROUPS, :], in_=mask.rearrange("b (g n) -> (b g) n", g=GROUPS)
-                    )
-            load_queries(b, 1)
-            nc.sync.dma_start(out=v_sb[:, b, :, :, :], in_=v_s[b, 0].rearrange("(g p t) d -> p g t d", p=P, t=PACK))
-            for c in range(2, CHUNKS):
-                load_queries(b, c)
+        nc.gpsimd.memset(columns[:], 0.0)
+        load_queries(0, 0, 1)
+        load_keys(0, 0, 1)
+        nc.sync.dma_start(out=mask_sb[0 : BATCH * GROUPS, :], in_=mask.rearrange("b (g n) -> (b g) n", g=GROUPS))
+        for g in range(1, GROUPS):
+            load_keys(0, g, g + 1)
+        load_queries(0, 1, 2)
+        load_values(0)
+        load_queries(0, 2, CHUNKS)
+
+        def load_second_batch():
+            load_keys(1, 0, GROUPS)
+            load_queries(1, 0, CHUNKS)
+            load_values(1)
+
+        load_second_batch()
 
         make_identity(nc, identity[:])
         make_identity(nc, identity_f32[:])
@@ -144,8 +168,12 @@ def tile_softmaxattention_kde_pa_kernel(tc, q_s, k_s, v_s, mask, out):
             kind, b, n = block
             return q_flipped[:, b, n, :] if kind == "q" else k_flipped[:, b, n, :]
 
-        def flip(block):
-            turned = prep_psum.tile([P, PACK, P], BF16, tag="prep")
+        def ring(engine):
+            return (score_psum, "scores") if engine == "v" else (prep_psum, "prep")
+
+        def flip(block, engine="v"):
+            pool, tag = ring(engine)
+            turned = pool.tile([P, PACK, P], BF16, tag=tag, name="turned")
             for a in range(PACK):
                 nc.tensor.transpose(turned[:, a, :], raw(block)[:, a, :], identity[:])
             prep[("flip", block)] = turned[:].rearrange("p a j -> p (a j)")
@@ -156,63 +184,48 @@ def tile_softmaxattention_kde_pa_kernel(tc, q_s, k_s, v_s, mask, out):
         def query_bias_by_vector(block):
             kind, b, n = block
             for a in range(Q_TILES):
-                unused = unused_pool.tile([P, DIM], F32)
+                unused = unused_pool.tile([P, DIM], F32, name="unused_1")
                 nc.vector.scalar_tensor_tensor(
                     out=unused[:],
                     in0=raw(block)[:, a, :],
-                    scalar=-0.5,
+                    scalar=0.5,
                     in1=raw(block)[:, a, :],
                     op0=ALU.mult,
                     op1=ALU.mult,
                     accum_out=q_column[:, b, n, a : a + 1],
                 )
 
+        def squares_by_vector(block):
+            kind, b, n = block
+            for t in range(PACK):
+                unused = unused_pool.tile([P, DIM], F32, name="unused_2")
+                nc.vector.scalar_tensor_tensor(
+                    out=unused[:],
+                    in0=raw(block)[:, t, :],
+                    scalar=0.5,
+                    in1=raw(block)[:, t, :],
+                    op0=ALU.mult,
+                    op1=ALU.mult,
+                    accum_out=k_square[:, b, n, t : t + 1],
+                )
+
         def squares_by_scalar(block):
             kind, b, n = block
-            total = q_square if kind == "q" else k_square
+            total = q_column if kind == "q" else k_square
             for t in range(PACK):
-                unused = unused_pool.tile([P, DIM], F32)
+                unused = unused_pool.tile([P, DIM], F32, name="unused_3")
                 nc.scalar.activation(
-                    out=unused[:], in_=raw(block)[:, t, :], func=ACT.Square, accum_out=total[:, b, n, t : t + 1]
+                    out=unused[:],
+                    in_=raw(block)[:, t, :],
+                    func=ACT.Square,
+                    scale=ROOT_HALF,
+                    accum_out=total[:, b, n, t : t + 1],
                 )
 
-        def bias_from_squares(block):
+        def add_mask(block):
             kind, b, n = block
-            if kind == "q":
-                nc.vector.tensor_scalar(
-                    out=q_column[:, b, n, :], in0=q_square[:, b, n, :], scalar1=-0.5, scalar2=None, op0=ALU.mult
-                )
-            else:
-                nc.vector.scalar_tensor_tensor(
-                    out=k_column[:, b, n, :],
-                    in0=k_square[:, b, n, :],
-                    scalar=-0.5,
-                    in1=mask_term[:, b, n, :],
-                    op0=ALU.mult,
-                    op1=ALU.add,
-                )
-
-        def query_bias_by_gpsimd(block):
-            kind, b, n = block
-            tree = tree_pool.tile([P, Q_TILES, 2 * DIM], F32)
-            nc.gpsimd.tensor_tensor(out=tree[:, :, 0:DIM], in0=raw(block), in1=raw(block), op=ALU.mult)
-            start, width = 0, DIM
-            while width > 1:
-                half = width // 2
-                nc.gpsimd.tensor_tensor(
-                    out=tree[:, :, start + width : start + width + half],
-                    in0=tree[:, :, start : start + half],
-                    in1=tree[:, :, start + half : start + width],
-                    op=ALU.add,
-                )
-                start, width = start + width, half
-            nc.gpsimd.tensor_scalar(
-                out=q_column[:, b, n, :],
-                in0=tree[:, :, start],
-                scalar1=-0.5,
-                scalar2=0.0,
-                op0=ALU.mult,
-                op1=ALU.add,
+            nc.vector.tensor_tensor(
+                out=k_column[:, b, n, :], in0=k_square[:, b, n, :], in1=mask_term[:, b, n, :], op=ALU.add
             )
 
         def is_in_fold(block):
@@ -228,7 +241,7 @@ def tile_softmaxattention_kde_pa_kernel(tc, q_s, k_s, v_s, mask, out):
         def fill_terms():
             for terms, first_one in ((k_terms[:], PARTS), (q_terms[:].rearrange("p c a j -> p (c a) j"), 0)):
                 nc.gpsimd.memset(terms, 0.0)
-                nc.gpsimd.memset(terms[:, :, first_one : first_one + PARTS], 1.0)
+                nc.gpsimd.memset(terms[:, :, first_one : first_one + PARTS], -1.0)
 
         def split(block):
             left, parts = terms_of(block)[:2]
@@ -239,9 +252,10 @@ def tile_softmaxattention_kde_pa_kernel(tc, q_s, k_s, v_s, mask, out):
                     nc.gpsimd.tensor_tensor(out=rest[:], in0=left, in1=parts[:, :, part], op=ALU.subtract)
                     left = rest[:]
 
-        def fold_flip(block):
+        def fold_flip(block, engine="v"):
             terms = terms_of(block)[2]
-            turned = prep_psum.tile([P, PACK, P], BF16, tag="prep", name="turned_terms")
+            pool, tag = ring(engine)
+            turned = pool.tile([P, PACK, P], BF16, tag=tag, name="turned_terms")
             for t in range(PACK):
                 nc.tensor.transpose(turned[:, t, :], terms[:, t, :], identity[:])
             prep[("fold", block)] = turned[:]
@@ -259,8 +273,33 @@ def tile_softmaxattention_kde_pa_kernel(tc, q_s, k_s, v_s, mask, out):
 
         def row_out(block, engine_copy):
             kind, b, n = block
-            target = q_row[:, b, n, :] if kind == "q" else k_row[:].rearrange("p t m -> p (t m)")
+            target = q_row[:, b, n, :] if kind == "q" else k_row[:, b, n, :, :].rearrange("p t m -> p (t m)")
             engine_copy(out=target, in_=prep[("row", block)])
+
+        parked = []
+
+        def turn_columns(b):
+            turned = prep_psum.tile([P, P], F32, tag="prep", name="turned_columns")
+            nc.tensor.transpose(turned[:], columns[:, b, :], identity_f32[:])
+            prep[("turn", b)] = turned
+
+        def turn_out(b, engine_copy):
+            k = len(parked) % 4
+            n = 4 * CHUNKS + 4 * GROUPS
+            engine_copy(out=row_parts[:, k, :], in_=prep[("turn", b)][0:n, :])
+            prep[("rows", b)] = row_parts[:, k, :]
+
+        def spread_rows(blocks):
+            spots = []
+            for kind, b, n in blocks:
+                first = 4 * n + (0 if kind == "q" else 4 * CHUNKS)
+                place = ALL_Q_TILES * len(parked) + ALL_Q_TILES - Q_TILES
+                parked.append((kind, b, n))
+                spots.append(out[BATCH - 1, 0, place : place + Q_TILES, :])
+                nc.sync.dma_start(out=spots[-1], in_=prep[("rows", b)][first : first + 4, :])
+            for (kind, b, n), spot in zip(blocks, spots):
+                target = q_row[:, b, n, :] if kind == "q" else k_row[:, b, n, :, :].rearrange("p t m -> p (t m)")
+                nc.sync.dma_start(out=target, in_=spot.rearrange("r d -> (r d)").partition_broadcast(P))
 
         def scores_to_logits(u, t, start, stop):
             b, c, g = unit_indices(u)
@@ -279,8 +318,8 @@ def tile_softmaxattention_kde_pa_kernel(tc, q_s, k_s, v_s, mask, out):
                 in0=scores[:, 0 : stop - start],
                 scalar=k_column[:, b, g, t : t + 1],
                 in1=q_row[:, b, c, start:stop],
-                op0=ALU.add,
-                op1=ALU.add,
+                op0=ALU.subtract,
+                op1=ALU.subtract,
             )
 
         def make_biases(u):
@@ -289,9 +328,9 @@ def tile_softmaxattention_kde_pa_kernel(tc, q_s, k_s, v_s, mask, out):
                 tile_biases = bias_pool.tile([P, PACK, P], F32)
                 nc.gpsimd.tensor_scalar(
                     out=tile_biases[:],
-                    in0=k_row[:],
+                    in0=k_row[:, b, g, :, :],
                     scalar1=q_column[:, b, c, a : a + 1],
-                    scalar2=1.0,
+                    scalar2=-1.0,
                     op0=ALU.add,
                     op1=ALU.mult,
                 )
@@ -430,50 +469,63 @@ def tile_softmaxattention_kde_pa_kernel(tc, q_s, k_s, v_s, mask, out):
         def queries_of(chunk):
             return ("q",) + divmod(chunk, CHUNKS)
 
-        def prepare(start, finish, block, engine_copy=nc.scalar.copy):
-            start(block)
-            finish(block, engine_copy)
+        def engine_copy(name):
+            return nc.scalar.copy if name == "s" else nc.vector.tensor_copy
 
-        def prepare_ahead(b, c, g):
-            chunk = b * CHUNKS + c
-            group = ("k", b + 1, (c + FOLD_GROUP) % GROUPS) if b + 1 < BATCH else None
-            copy = nc.scalar.copy if b == 0 else nc.vector.tensor_copy
+        def ahead(chunk, g, t):
+            b, c = divmod(chunk, CHUNKS)
             following = queries_of(chunk + 1) if chunk + 1 < BATCH * CHUNKS else None
-            if g == 0 and following:
-                prepare(flip, flip_out, following, copy)
-            if g == 0 and chunk < SUMMED_BY_SCALAR:
-                squares_by_scalar(queries_of(chunk + 2))
-            if g == 1 and chunk < SUMMED_BY_SCALAR:
-                bias_from_squares(queries_of(chunk + 2))
-            if g == 1 and group:
-                prepare(flip, flip_out, group)
-            if g == 2 and following:
-                prepare(row, row_out, following)
-            if g == 2 and group:
-                squares_by_scalar(group)
-            if g == 3 and group:
-                bias_from_squares(group)
-            if g == 3 and following and is_in_fold(following):
-                prepare(fold_flip, fold_out, following, copy)
-            if g == 3 and chunk == 1:
-                prepare(fold_flip, fold_out, ("k", 1, FOLD_GROUP))
-            if g == 1 and chunk == BATCH * CHUNKS - 2:
-                prepare(row, row_out, ("k", 1, FOLD_GROUP))
+            after = queries_of(chunk + 2) if chunk + 2 < BATCH * CHUNKS else None
+            group = ("k", b + 1, (c + FOLD_GROUP) % GROUPS) if b + 1 < BATCH else None
+            at = (g, t)
+            if following:
+                if at == FLIP_Q[0]:
+                    flip(following, FLIP_Q_BY[chunk])
+                    flip_out(following, engine_copy(FLIP_Q_BY[chunk]))
+            if group:
+                if at == FLIP_K[0]:
+                    flip(group, FLIP_K_BY[chunk])
+                    flip_out(group, engine_copy(FLIP_K_BY[chunk]))
+                if at == SQUARE_K[0]:
+                    (squares_by_scalar if SQUARE_K_BY[chunk] == "s" else squares_by_vector)(group)
+                if at == SQUARE_K[1]:
+                    add_mask(group)
+            if after:
+                if at == SQUARE_Q[0]:
+                    (squares_by_scalar if SQUARE_Q_BY[chunk] == "s" else query_bias_by_vector)(after)
+            if following and is_in_fold(following):
+                if at == FOLD_Q[0]:
+                    fold_flip(following, FOLD_BY[chunk])
+                    fold_out(following, engine_copy(FOLD_BY[chunk]))
+            if chunk == 1:
+                if at == FOLD_Q[0]:
+                    fold_flip(("k", 1, FOLD_GROUP), FOLD_BY[chunk])
+                    fold_out(("k", 1, FOLD_GROUP), engine_copy(FOLD_BY[chunk]))
+            for batch, first, second, blocks in TURNS.get(chunk, ()):
+                if at == first:
+                    turn_columns(batch)
+                    turn_out(batch, engine_copy("v"))
+                    spread_rows(blocks)
+            if chunk == 0 and at == FILL_AT:
+                for tg in TRANSPOSED[1]:
+                    make_biases(GROUPS + tg)
+                fill_terms()
 
         def gpsimd_work(chunk, g):
             b, c = divmod(chunk, CHUNKS)
             work = []
-            if g == 1 and SUMMED_BY_SCALAR <= chunk < BATCH * CHUNKS - 2:
-                work.append((query_bias_by_gpsimd, queries_of(chunk + 2)))
             if g == 1 and chunk < BATCH * CHUNKS - 2 and is_in_fold(queries_of(chunk + 2)):
                 work.append((split, queries_of(chunk + 2)))
             if g == 3 and chunk == 0:
                 work.append((group_values, 1))
             if g == 1 and chunk == 1:
                 work.append((split, ("k", 1, FOLD_GROUP)))
-            if g == 1 and chunk == BATCH * CHUNKS - 2:
-                work.append((make_biases, UNITS - 1))
-            if work:
+            if 0 < chunk < BATCH * CHUNKS - 1:
+                ahead_groups = TRANSPOSED[chunk + 1]
+                for k, tg in enumerate(ahead_groups):
+                    if g == (1 if k == 0 else 3):
+                        work.append((make_biases, (chunk + 1) * GROUPS + tg))
+            if work and chunk:
                 scales = packed[unit_of_last_quantise[0]][1]
                 nc.gpsimd.tensor_copy(out=seen[:], in_=scales[:, unit_of_last_quantise[1], 0:PACK])
             for task, argument in work:
@@ -486,26 +538,25 @@ def tile_softmaxattention_kde_pa_kernel(tc, q_s, k_s, v_s, mask, out):
             nc.vector.tensor_scalar(
                 out=mask_term[:].rearrange("p b g t -> p (b g) t"),
                 in0=turned[:, :, 0 : BATCH * GROUPS].rearrange("p t g -> p g t"),
-                scalar1=MASK_BIAS,
-                scalar2=-MASK_BIAS,
+                scalar1=-MASK_BIAS,
+                scalar2=MASK_BIAS,
                 op0=ALU.mult,
                 op1=ALU.add,
             )
 
-        query_bias_by_vector(q0)
-        squares_by_scalar(k0)
+        squares_by_scalar(q0)
         flip(q0)
         flip(k0)
-        flip_out(q0, nc.vector.tensor_copy)
         row(q0)
-        row_out(q0, nc.scalar.copy)
+        flip_out(q0, nc.vector.tensor_copy)
+        squares_by_scalar(k0)
         flip_out(k0, nc.vector.tensor_copy)
         spread_mask()
-        bias_from_squares(k0)
+        row_out(q0, nc.scalar.copy)
+        add_mask(k0)
         squares_by_scalar(k1)
         flip(k1)
         flip_out(k1, nc.vector.tensor_copy)
-        fill_terms()
         group_values(0)
 
         for u in range(UNITS):
@@ -514,36 +565,43 @@ def tile_softmaxattention_kde_pa_kernel(tc, q_s, k_s, v_s, mask, out):
             for t in range(PACK):
                 if t == FOLD_SLOT and is_folded_by_parts(b, c, FOLD_GROUP):
                     folded_tile_by_parts(u - g + FOLD_GROUP, g)
-                if is_folded_by_transposes(b, c, FOLD_GROUP) and (g, t) in LAST_FOLD_SLOTS:
-                    folded_tile_by_transposes(UNITS - 1, LAST_FOLD_SLOTS.index((g, t)))
+                chunk = u // GROUPS
+                tiles = [(tg, a) for tg in TRANSPOSED[chunk] for a in range(Q_TILES)]
+                if chunk == BATCH * CHUNKS - 1 and len(tiles) == 4:
+                    slots = LAST_FOLD_SLOTS
+                else:
+                    slots = FOLD_SLOTS if len(tiles) == 4 else FOLD_SLOTS2
+                if tiles and (g, t) in slots:
+                    tg, a = tiles[slots.index((g, t))]
+                    folded_tile_by_transposes(u - g + tg, a)
                 if u == LAST_SUBTRACTED:
                     for t2 in (2 * t % PACK, 2 * t % PACK + 1):
                         scores_to_logits(u, t2, t // 2 * (CHUNK // 2), (t // 2 + 1) * (CHUNK // 2))
                 elif not is_folded(b, c, g):
                     scores_to_logits(u, t, 0, CHUNK)
-                if t == PREPARE_SLOT:
-                    prepare_ahead(b, c, g)
+                ahead(u // GROUPS, g, t)
                 if u == 0 and t == 1:
                     squares_by_scalar(k2)
-                    flip(k2)
-                    flip_out(k2, nc.vector.tensor_copy)
-                    bias_from_squares(k1)
-                if u == 1 and t == 0:
-                    bias_from_squares(k3)
-                    bias_from_squares(q1)
-                if u == 0 and t == 3:
                     squares_by_scalar(k3)
                     squares_by_scalar(q1)
+                    flip(k2)
+                    flip_out(k2, nc.vector.tensor_copy)
+                    add_mask(k1)
+                if u == 0 and t == 3:
                     flip(k3)
                     flip_out(k3, nc.vector.tensor_copy)
-                    bias_from_squares(k2)
-            if u == 3:
+                    add_mask(k2)
+                    add_mask(k3)
+            if u == VALUES_AT:
                 quantise_values(0)
             if u == 2 * GROUPS:
                 quantise_values(1)
             if u % 2 == 1 and u > 1:
-                quantise_pair(u - 2)
+                if u > 3:
+                    quantise_pair(u - 2)
                 gpsimd_work(b * CHUNKS + c, g)
+            if u == FIRST_QUANT:
+                quantise_pair(1)
             done = u // GROUPS - 1
             if done >= 0 and g == 2:
                 sums[done] = out_psum.tile([P, Q_TILES, DIM], F32, name="acc")
@@ -551,7 +609,7 @@ def tile_softmaxattention_kde_pa_kernel(tc, q_s, k_s, v_s, mask, out):
                     attn_times_values(done // CHUNKS, done % CHUNKS, a, sums[done][:, a, :])
             if done >= 0 and g == 3:
                 result = result_pool.tile([P, Q_TILES, DIM], F32)
-                (nc.vector.tensor_copy if last else nc.scalar.copy)(out=result[:], in_=sums[done][:])
+                engine_copy(RESULT_BY[done])(out=result[:], in_=sums[done][:])
                 store(done // CHUNKS, done % CHUNKS, 0, Q_TILES, result[:])
             if u != LAST_SUBTRACTED and not is_folded(b, c, g):
                 exponentials(u)

@@ -30,7 +30,9 @@ RUN = 4
 FOLD_GROUP = GROUPS - 1
 FOLD_SLOT = 3
 TRANSPOSED = ((), (3,), (3,), (3,), (), (), (), (3,))
-TURNS = {0: ((0, (1, 2), (1, 3), (("k", 0, 3), ("q", 0, 1))), (0, (3, 2), (3, 3), (("q", 0, 2),))), 1: ((0, (2, 2), (2, 3), (("q", 0, 3),)),), 2: ((1, (2, 2), (2, 3), (("q", 1, 0),)),), 3: ((1, (2, 2), (2, 3), (("q", 1, 1),)),), 4: ((1, (2, 2), (2, 3), (("q", 1, 2), ("k", 1, 3))),), 5: ((1, (2, 2), (2, 3), (("q", 1, 3),)),)}
+TURNS = {0: ((0, (3, 2), (3, 3), (("q", 0, 2),)),), 1: ((0, (2, 2), (2, 3), (("q", 0, 3),)),), 2: ((1, (2, 2), (2, 3), (("q", 1, 0),)),), 3: ((1, (2, 2), (2, 3), (("q", 1, 1),)),), 4: ((1, (2, 2), (2, 3), (("q", 1, 2), ("k", 1, 3))),), 5: ((1, (2, 2), (2, 3), (("q", 1, 3),)),)}
+FIRST_ROWS = ((1, 1), (2, 1))
+FIRST_ROW_BY = "s"
 FILL_AT = (2, 3)
 VALUES_AT = 5
 FIRST_QUANT = 4
@@ -39,7 +41,7 @@ FLIP_K_BY = "vvvvvvvv"
 SQUARE_Q_BY = "ssssssss"
 SQUARE_K_BY = "ssssssss"
 FOLD_BY = "vvvvvvvv"
-RESULT_BY = "ssssssss"
+RESULT_BY = "svssssss"
 FLIP_Q = ((1, 1), (0, 3))
 FLIP_K = ((1, 3), (1, 3))
 SQUARE_Q = ((0, 2), (1, 1))
@@ -506,6 +508,12 @@ def tile_softmaxattention_kde_pa_kernel(tc, q_s, k_s, v_s, mask, out):
                     turn_columns(batch)
                     turn_out(batch, engine_copy("v"))
                     spread_rows(blocks)
+            if chunk == 0 and at == FIRST_ROWS[0]:
+                row(("k", 0, FOLD_GROUP))
+                row_out(("k", 0, FOLD_GROUP), nc.scalar.copy)
+            if chunk == 0 and at == FIRST_ROWS[1]:
+                row(("q", 0, 1))
+                row_out(("q", 0, 1), engine_copy(FIRST_ROW_BY))
             if chunk == 0 and at == FILL_AT:
                 for tg in TRANSPOSED[1]:
                     make_biases(GROUPS + tg)
@@ -551,8 +559,8 @@ def tile_softmaxattention_kde_pa_kernel(tc, q_s, k_s, v_s, mask, out):
         flip_out(q0, nc.vector.tensor_copy)
         squares_by_scalar(k0)
         flip_out(k0, nc.vector.tensor_copy)
+        row_out(q0, nc.vector.tensor_copy)
         spread_mask()
-        row_out(q0, nc.scalar.copy)
         add_mask(k0)
         squares_by_scalar(k1)
         flip(k1)

@@ -384,8 +384,8 @@ def tile_softmaxattention_kde_pa_kernel(tc, q_s, k_s, v_s, mask, out):
 
         def folded_exp(u, a, bank):
             nc.scalar.activation(
-                out=attn_of(u)[:, a * P : (a + 1) * P, :],
-                in_=bank[:].rearrange("p t n -> p n t"),
+                out=attn_of(u)[:, a * P : (a + 1) * P, :].rearrange("p (c i) t -> p c t i", i=RUN),
+                in_=bank[:].rearrange("p t (c i) -> p c t i", i=RUN),
                 func=ACT.Exp,
             )
 

@@ -25,7 +25,7 @@ ALL_Q_TILES = TOKENS // P
 UNITS = BATCH * CHUNKS * GROUPS
 MASK_BIAS = 1.0e9
 ROOT_HALF = 0.5**0.5
-RUN = 4
+RUN = 2
 
 FOLD_GROUP = GROUPS - 1
 FOLD_SLOT = 3

from contextlib import ExitStack

import concourse.mybir as mybir
from concourse.masks import make_identity

F32 = mybir.dt.float32
BF16 = mybir.dt.bfloat16
U32 = mybir.dt.uint32
U8 = mybir.dt.uint8
FP8X4 = mybir.dt.float8_e4m3fn_x4
ALU = mybir.AluOpType
ACT = mybir.ActivationFunctionType

P = 128
PACK = 4
BATCH = 2
TOKENS = 2048
DIM = 128
GROUP = P * PACK
GROUPS = TOKENS // GROUP
CHUNK = 512
CHUNKS = TOKENS // CHUNK
Q_TILES = CHUNK // P
ALL_Q_TILES = TOKENS // P
UNITS = BATCH * CHUNKS * GROUPS
MASK_BIAS = 1.0e9
ROOT_HALF = 0.5**0.5
RUN = 2

FOLD_GROUP = GROUPS - 1
FOLD_SLOT = 3
TRANSPOSED = ((), (3,), (3,), (3,), (), (), (), (3,))
TURNS = {0: ((0, (3, 2), (3, 3), (("q", 0, 2),)),), 1: ((0, (2, 2), (2, 3), (("q", 0, 3),)),), 2: ((1, (2, 2), (2, 3), (("q", 1, 0),)),), 3: ((1, (2, 2), (2, 3), (("q", 1, 1),)),), 4: ((1, (2, 2), (2, 3), (("q", 1, 2), ("k", 1, 3))),), 5: ((1, (2, 2), (2, 3), (("q", 1, 3),)),)}
FIRST_ROWS = ((1, 1), (2, 1))
FIRST_ROW_BY = "s"
FILL_AT = (2, 3)
VALUES_AT = 5
FIRST_QUANT = 4
FLIP_Q_BY = "vvvvvvvv"
FLIP_K_BY = "vvvvvvvv"
SQUARE_Q_BY = "ssssssss"
SQUARE_K_BY = "ssssssss"
FOLD_BY = "vvvvvvvv"
RESULT_BY = "svssssss"
FLIP_Q = ((1, 1), (0, 3))
FLIP_K = ((1, 3), (1, 3))
SQUARE_Q = ((0, 2), (1, 1))
SQUARE_K = ((2, 2), (3, 1))
FOLD_Q = ((3, 1), (3, 3))
LAST_FOLD_SLOTS = ((0, 3), (1, 3), (2, 0), (2, 1))
FOLD_SLOTS = ((0, 3), (1, 3), (2, 3), (3, 3))
FOLD_SLOTS2 = ((0, 1), (0, 3), (1, 1), (1, 3), (2, 1), (2, 3), (3, 1), (3, 3))
LAST_SUBTRACTED = UNITS - 2
PARTS = 3

FLOPS = 2 * (2 * BATCH * TOKENS * TOKENS * DIM)


def unit_indices(u):
    return u // (CHUNKS * GROUPS), (u // GROUPS) % CHUNKS, u % GROUPS


def is_folded_by_parts(b, c, g):
    return b == BATCH - 1 and c < CHUNKS - 1 and g == FOLD_GROUP


def is_folded_by_transposes(b, c, g):
    return g in TRANSPOSED[b * CHUNKS + c]


def is_folded(b, c, g):
    return is_folded_by_parts(b, c, g) or is_folded_by_transposes(b, c, g)


def tile_softmaxattention_kde_pa_kernel(tc, q_s, k_s, v_s, mask, out):
    nc = tc.nc
    with ExitStack() as ctx:
        keep = ctx.enter_context(tc.tile_pool(name="keep", bufs=1))
        bias_pool = ctx.enter_context(tc.tile_pool(name="bias", bufs=16))
        rest_pool = ctx.enter_context(tc.tile_pool(name="rest", bufs=4))
        unused_pool = ctx.enter_context(tc.tile_pool(name="unused", bufs=4))
        logits_pool = ctx.enter_context(tc.tile_pool(name="logits", bufs=4))
        attn_pool = ctx.enter_context(tc.tile_pool(name="attn", bufs=4))
        packed_pool = ctx.enter_context(tc.tile_pool(name="packed", bufs=2))
        result_pool = ctx.enter_context(tc.tile_pool(name="result", bufs=4))
        score_psum = ctx.enter_context(tc.psum_pool(name="score_psum", bufs=4))
        prep_psum = ctx.enter_context(tc.psum_pool(name="prep_psum", bufs=3))
        out_psum = ctx.enter_context(tc.psum_pool(name="out_psum", bufs=1))
        ctx.enter_context(tc.manual_schedule())

        q_raw = keep.tile([P, BATCH, CHUNKS, Q_TILES, DIM], BF16)
        k_raw = keep.tile([P, BATCH, GROUPS, PACK, DIM], BF16)
        q_flipped = keep.tile([P, BATCH, CHUNKS, CHUNK], BF16)
        k_flipped = keep.tile([P, BATCH, GROUPS, GROUP], BF16)
        k_square = keep.tile([P, BATCH, GROUPS, PACK], F32)
        k_terms = keep.tile([P, PACK, P], BF16)
        q_terms = keep.tile([P, CHUNKS, Q_TILES, P], BF16)
        k_folds = keep.tile([P, PACK, P], BF16)
        q_folds = keep.tile([P, CHUNKS, Q_TILES, P], BF16)
        columns = keep.tile([P, BATCH, P], F32)
        row_parts = keep.tile([4 * CHUNKS + 4 * GROUPS, 4, P], F32)
        q_column = columns[:, :, 0 : CHUNKS * Q_TILES].rearrange("p b (c a) -> p b c a", a=Q_TILES)
        k_column = columns[:, :, CHUNKS * Q_TILES : CHUNKS * Q_TILES + GROUPS * PACK].rearrange("p b (g t) -> p b g t", t=PACK)
        q_row = keep.tile([P, BATCH, CHUNKS, CHUNK], F32)
        k_row = keep.tile([P, BATCH, GROUPS, PACK, P], F32)
        mask_sb = keep.tile([P, GROUP], BF16)
        mask_term = keep.tile([P, BATCH, GROUPS, PACK], F32)
        v_sb = keep.tile([P, BATCH, GROUPS, PACK, DIM], BF16)
        v_grouped = keep.tile([P, BATCH, GROUPS, DIM, PACK], BF16, align_bytes=64)
        v_codes = keep.tile([P, BATCH, GROUPS, DIM], U32, align_bytes=64)
        v_scales = keep.tile([P, BATCH, GROUPS, DIM], U8, align_bytes=64)
        identity = keep.tile([P, P], BF16)
        identity_f32 = keep.tile([P, P], F32)
        warm = keep.tile([P, 1], F32)
        seen = keep.tile([P, PACK], U8)

        def load_queries(b, c0, c1):
            nc.sync.dma_start(
                out=q_raw[:, b, c0:c1, :, :],
                in_=q_s[b, 0].rearrange("(j c a) d -> j c a d", c=CHUNKS, a=Q_TILES)[:, c0:c1, :, :],
            )

        def load_keys(b, g0, g1):
            nc.sync.dma_start(
                out=k_raw[:, b, g0:g1, :, :],
                in_=k_s[b, 0].rearrange("(g p t) d -> p g t d", p=P, t=PACK)[:, g0:g1, :, :],
            )

        def load_values(b):
            nc.sync.dma_start(out=v_sb[:, b, :, :, :], in_=v_s[b, 0].rearrange("(g p t) d -> p g t d", p=P, t=PACK))

        nc.gpsimd.memset(mask_sb[:].bitcast(U32), 0)
        nc.gpsimd.memset(columns[:], 0.0)
        load_queries(0, 0, 1)
        load_keys(0, 0, 1)
        nc.sync.dma_start(out=mask_sb[0 : BATCH * GROUPS, :], in_=mask.rearrange("b (g n) -> (b g) n", g=GROUPS))
        for g in range(1, GROUPS):
            load_keys(0, g, g + 1)
        load_queries(0, 1, 2)
        load_values(0)
        load_queries(0, 2, CHUNKS)

        def load_second_batch():
            load_keys(1, 0, GROUPS)
            load_queries(1, 0, CHUNKS)
            load_values(1)

        load_second_batch()

        make_identity(nc, identity[:])
        make_identity(nc, identity_f32[:])
        nc.vector.memset(warm[:], 0.0)
        nc.scalar.activation(out=warm[:], in_=warm[:], func=ACT.Exp)
        prep = {}

        unit_of_last_quantise = [None, None]
        biases = {}
        logits = {}
        attn = {}
        packed = {}
        sums = {}

        q0, q1, k0, k1, k2, k3 = [("q", 0, 0), ("q", 0, 1)] + [("k", 0, g) for g in range(GROUPS)]

        def raw(block):
            kind, b, n = block
            return q_raw[:, b, n, :, :] if kind == "q" else k_raw[:, b, n, :, :]

        def flipped(block):
            kind, b, n = block
            return q_flipped[:, b, n, :] if kind == "q" else k_flipped[:, b, n, :]

        def ring(engine):
            return (score_psum, "scores") if engine == "v" else (prep_psum, "prep")

        def flip(block, engine="v"):
            pool, tag = ring(engine)
            turned = pool.tile([P, PACK, P], BF16, tag=tag, name="turned")
            for a in range(PACK):
                nc.tensor.transpose(turned[:, a, :], raw(block)[:, a, :], identity[:])
            prep[("flip", block)] = turned[:].rearrange("p a j -> p (a j)")

        def flip_out(block, engine_copy):
            engine_copy(out=flipped(block), in_=prep[("flip", block)])

        def query_bias_by_vector(block):
            kind, b, n = block
            for a in range(Q_TILES):
                unused = unused_pool.tile([P, DIM], F32, name="unused_1")
                nc.vector.scalar_tensor_tensor(
                    out=unused[:],
                    in0=raw(block)[:, a, :],
                    scalar=0.5,
                    in1=raw(block)[:, a, :],
                    op0=ALU.mult,
                    op1=ALU.mult,
                    accum_out=q_column[:, b, n, a : a + 1],
                )

        def squares_by_vector(block):
            kind, b, n = block
            for t in range(PACK):
                unused = unused_pool.tile([P, DIM], F32, name="unused_2")
                nc.vector.scalar_tensor_tensor(
                    out=unused[:],
                    in0=raw(block)[:, t, :],
                    scalar=0.5,
                    in1=raw(block)[:, t, :],
                    op0=ALU.mult,
                    op1=ALU.mult,
                    accum_out=k_square[:, b, n, t : t + 1],
                )

        def squares_by_scalar(block):
            kind, b, n = block
            total = q_column if kind == "q" else k_square
            for t in range(PACK):
                unused = unused_pool.tile([P, DIM], F32, name="unused_3")
                nc.scalar.activation(
                    out=unused[:],
                    in_=raw(block)[:, t, :],
                    func=ACT.Square,
                    scale=ROOT_HALF,
                    accum_out=total[:, b, n, t : t + 1],
                )

        def add_mask(block):
            kind, b, n = block
            nc.vector.tensor_tensor(
                out=k_column[:, b, n, :], in0=k_square[:, b, n, :], in1=mask_term[:, b, n, :], op=ALU.add
            )

        def is_in_fold(block):
            kind, b, n = block
            return is_folded_by_parts(b, n, FOLD_GROUP) if kind == "q" else is_folded_by_parts(b, 0, n)

        def terms_of(block):
            kind, b, n = block
            if kind == "k":
                return k_column[:, b, n, :], k_terms[:, :, 0:PARTS], k_terms[:], k_folds[:]
            return q_column[:, b, n, :], q_terms[:, n, :, PARTS : 2 * PARTS], q_terms[:, n, :, :], q_folds[:, n, :, :]

        def fill_terms():
            for terms, first_one in ((k_terms[:], PARTS), (q_terms[:].rearrange("p c a j -> p (c a) j"), 0)):
                nc.gpsimd.memset(terms, 0.0)
                nc.gpsimd.memset(terms[:, :, first_one : first_one + PARTS], -1.0)

        def split(block):
            left, parts = terms_of(block)[:2]
            for part in range(PARTS):
                nc.gpsimd.tensor_copy(out=parts[:, :, part], in_=left)
                if part + 1 < PARTS:
                    rest = rest_pool.tile([P, PACK], F32)
                    nc.gpsimd.tensor_tensor(out=rest[:], in0=left, in1=parts[:, :, part], op=ALU.subtract)
                    left = rest[:]

        def fold_flip(block, engine="v"):
            terms = terms_of(block)[2]
            pool, tag = ring(engine)
            turned = pool.tile([P, PACK, P], BF16, tag=tag, name="turned_terms")
            for t in range(PACK):
                nc.tensor.transpose(turned[:, t, :], terms[:, t, :], identity[:])
            prep[("fold", block)] = turned[:]

        def fold_out(block, engine_copy):
            engine_copy(out=terms_of(block)[3], in_=prep[("fold", block)])

        def row(block):
            kind, b, n = block
            column = q_column if kind == "q" else k_column
            rows = (score_psum if block == q0 else prep_psum).tile([P, Q_TILES, P], F32, tag="scores" if block == q0 else "prep", name="rows")
            for a in range(Q_TILES):
                nc.tensor.transpose(rows[:, a, :], column[:, b, n, a : a + 1].to_broadcast([P, P]), identity_f32[:])
            prep[("row", block)] = rows[:].rearrange("p a n -> p (a n)")

        def row_out(block, engine_copy):
            kind, b, n = block
            target = q_row[:, b, n, :] if kind == "q" else k_row[:, b, n, :, :].rearrange("p t m -> p (t m)")
            engine_copy(out=target, in_=prep[("row", block)])

        parked = []

        def turn_columns(b):
            turned = prep_psum.tile([P, P], F32, tag="prep", name="turned_columns")
            nc.tensor.transpose(turned[:], columns[:, b, :], identity_f32[:])
            prep[("turn", b)] = turned

        def turn_out(b, engine_copy):
            k = len(parked) % 4
            n = 4 * CHUNKS + 4 * GROUPS
            engine_copy(out=row_parts[:, k, :], in_=prep[("turn", b)][0:n, :])
            prep[("rows", b)] = row_parts[:, k, :]

        def spread_rows(blocks):
            spots = []
            for kind, b, n in blocks:
                first = 4 * n + (0 if kind == "q" else 4 * CHUNKS)
                place = ALL_Q_TILES * len(parked) + ALL_Q_TILES - Q_TILES
                parked.append((kind, b, n))
                spots.append(out[BATCH - 1, 0, place : place + Q_TILES, :])
                nc.sync.dma_start(out=spots[-1], in_=prep[("rows", b)][first : first + 4, :])
            for (kind, b, n), spot in zip(blocks, spots):
                target = q_row[:, b, n, :] if kind == "q" else k_row[:, b, n, :, :].rearrange("p t m -> p (t m)")
                nc.sync.dma_start(out=target, in_=spot.rearrange("r d -> (r d)").partition_broadcast(P))

        def scores_to_logits(u, t, start, stop):
            b, c, g = unit_indices(u)
            if u not in logits:
                logits[u] = logits_pool.tile([P, PACK, CHUNK], F32, name="unit_logits")
            scores = score_psum.tile([P, CHUNK], F32, tag="scores")
            nc.tensor.matmul(
                out=scores[:, 0 : stop - start],
                lhsT=k_flipped[:, b, g, t * P : (t + 1) * P],
                rhs=q_flipped[:, b, c, start:stop],
                start=True,
                stop=True,
            )
            nc.vector.scalar_tensor_tensor(
                out=logits[u][:, t, start:stop],
                in0=scores[:, 0 : stop - start],
                scalar=k_column[:, b, g, t : t + 1],
                in1=q_row[:, b, c, start:stop],
                op0=ALU.subtract,
                op1=ALU.subtract,
            )

        def make_biases(u):
            b, c, g = unit_indices(u)
            for a in range(Q_TILES):
                tile_biases = bias_pool.tile([P, PACK, P], F32)
                nc.gpsimd.tensor_scalar(
                    out=tile_biases[:],
                    in0=k_row[:, b, g, :, :],
                    scalar1=q_column[:, b, c, a : a + 1],
                    scalar2=-1.0,
                    op0=ALU.add,
                    op1=ALU.mult,
                )
                biases[(u, a)] = tile_biases

        def folded_tile_by_transposes(u, a):
            b, c, g = unit_indices(u)
            queries = slice(a * P, (a + 1) * P)
            bank = prep_psum.tile([P, PACK, P], F32, tag="prep", name="bank")
            for t in range(PACK):
                nc.tensor.matmul(
                    out=bank[:, t, :],
                    lhsT=biases[(u, a)][:, t, :],
                    rhs=identity_f32[:],
                    is_transpose=True,
                    start=(t == 0),
                    stop=False,
                )
            for t in range(PACK):
                nc.tensor.matmul(
                    out=bank[:, t, :],
                    lhsT=k_flipped[:, b, g, t * P : (t + 1) * P],
                    rhs=q_flipped[:, b, c, queries],
                    start=False,
                    stop=(t == PACK - 1),
                )
            folded_exp(u, a, bank)

        def folded_tile_by_parts(u, a):
            b, c, g = unit_indices(u)
            queries = slice(a * P, (a + 1) * P)
            bank = prep_psum.tile([P, PACK, P], F32, tag="prep", name="bank")
            for t in range(PACK):
                nc.tensor.matmul(
                    out=bank[:, t, :],
                    lhsT=k_flipped[:, b, g, t * P : (t + 1) * P],
                    rhs=q_flipped[:, b, c, queries],
                    start=True,
                    stop=False,
                )
                nc.tensor.matmul(
                    out=bank[:, t, :],
                    lhsT=k_folds[:, t, :],
                    rhs=q_folds[:, c, a, :],
                    start=False,
                    stop=True,
                )
            folded_exp(u, a, bank)

        def folded_exp(u, a, bank):
            nc.scalar.activation(
                out=attn_of(u)[:, a * P : (a + 1) * P, :].rearrange("p (c i) t -> p c t i", i=RUN),
                in_=bank[:].rearrange("p t (c i) -> p c t i", i=RUN),
                func=ACT.Exp,
            )

        def attn_of(u):
            if u // 2 not in attn:
                attn[u // 2] = attn_pool.tile([P, 2, CHUNK, PACK], BF16, align_bytes=64, name="pair_attn")
            return attn[u // 2][:, u % 2, :, :]

        def exponentials(u, a0=0, a1=Q_TILES):
            queries = slice(a0 * P, a1 * P)
            nc.scalar.activation(
                out=attn_of(u)[:, queries, :].rearrange("p (c i) t -> p c t i", i=RUN),
                in_=logits[u][:, :, queries].rearrange("p t (c i) -> p c t i", i=RUN),
                func=ACT.Exp,
            )

        def group_values(b):
            for g in range(GROUPS):
                nc.gpsimd.tensor_scalar(
                    out=v_grouped[:, b, g, :, :],
                    in0=v_sb[:, b, g, :, :].rearrange("p t d -> p d t"),
                    scalar1=1.0,
                    scalar2=0.0,
                    op0=ALU.mult,
                    op1=ALU.add,
                )

        def quantise_values(b):
            nc.vector.quantize_mx(
                out=v_codes[:, b, :, :].rearrange("p g d -> p (g d)").bitcast(FP8X4),
                scales=v_scales[:, b, :, :].rearrange("p g d -> p (g d)"),
                in_=v_grouped[:, b, :, :, :].rearrange("p g d t -> p (g d t)"),
            )

        def packed_of(b, c):
            if (b, c) not in packed:
                codes = packed_pool.tile([P, GROUPS, CHUNK], U32, align_bytes=64)
                scales = packed_pool.tile([P, GROUPS, CHUNK], U8, align_bytes=64)
                packed[(b, c)] = (codes, scales)
            return packed[(b, c)]

        def quantise_pair(u):
            b, c, g = unit_indices(u)
            codes, scales = packed_of(b, c)
            nc.vector.quantize_mx(
                out=codes[:, g - 1 : g + 1, :].rearrange("p g n -> p (g n)").bitcast(FP8X4),
                scales=scales[:, g - 1 : g + 1, :].rearrange("p g n -> p (g n)"),
                in_=attn[u // 2][:].rearrange("p g n t -> p (g n t)"),
            )
            unit_of_last_quantise[:] = [(b, c), g]

        def quantise_part(u, a0, a1):
            b, c, g = unit_indices(u)
            codes, scales = packed_of(b, c)
            queries = slice(a0 * P, a1 * P)
            nc.vector.quantize_mx(
                out=codes[:, g, queries].bitcast(FP8X4),
                scales=scales[:, g, queries],
                in_=attn_of(u)[:, queries, :].rearrange("p n t -> p (n t)"),
            )

        def attn_times_values(b, c, a, acc):
            codes, scales = packed[(b, c)]
            queries = slice(a * P, (a + 1) * P)
            for g in range(GROUPS):
                nc.tensor.matmul_mx(
                    out=acc,
                    lhsT=codes[:, g, queries].bitcast(FP8X4),
                    lhsT_scale=scales[:, g, queries],
                    rhs=v_codes[:, b, g, :].bitcast(FP8X4),
                    rhs_scale=v_scales[:, b, g, :],
                    start=(g == 0),
                    stop=(g == GROUPS - 1),
                )

        def store(b, c, a0, a1, result):
            tiles = slice(c * Q_TILES + a0, c * Q_TILES + a1)
            nc.sync.dma_start(
                out=out[b, 0].rearrange("(j a) d -> j a d", a=ALL_Q_TILES)[:, tiles, :],
                in_=result,
            )

        def queries_of(chunk):
            return ("q",) + divmod(chunk, CHUNKS)

        def engine_copy(name):
            return nc.scalar.copy if name == "s" else nc.vector.tensor_copy

        def ahead(chunk, g, t):
            b, c = divmod(chunk, CHUNKS)
            following = queries_of(chunk + 1) if chunk + 1 < BATCH * CHUNKS else None
            after = queries_of(chunk + 2) if chunk + 2 < BATCH * CHUNKS else None
            group = ("k", b + 1, (c + FOLD_GROUP) % GROUPS) if b + 1 < BATCH else None
            at = (g, t)
            if following:
                if at == FLIP_Q[0]:
                    flip(following, FLIP_Q_BY[chunk])
                    flip_out(following, engine_copy(FLIP_Q_BY[chunk]))
            if group:
                if at == FLIP_K[0]:
                    flip(group, FLIP_K_BY[chunk])
                    flip_out(group, engine_copy(FLIP_K_BY[chunk]))
                if at == SQUARE_K[0]:
                    (squares_by_scalar if SQUARE_K_BY[chunk] == "s" else squares_by_vector)(group)
                if at == SQUARE_K[1]:
                    add_mask(group)
            if after:
                if at == SQUARE_Q[0]:
                    (squares_by_scalar if SQUARE_Q_BY[chunk] == "s" else query_bias_by_vector)(after)
            if following and is_in_fold(following):
                if at == FOLD_Q[0]:
                    fold_flip(following, FOLD_BY[chunk])
                    fold_out(following, engine_copy(FOLD_BY[chunk]))
            if chunk == 1:
                if at == FOLD_Q[0]:
                    fold_flip(("k", 1, FOLD_GROUP), FOLD_BY[chunk])
                    fold_out(("k", 1, FOLD_GROUP), engine_copy(FOLD_BY[chunk]))
            for batch, first, second, blocks in TURNS.get(chunk, ()):
                if at == first:
                    turn_columns(batch)
                    turn_out(batch, engine_copy("v"))
                    spread_rows(blocks)
            if chunk == 0 and at == FIRST_ROWS[0]:
                row(("k", 0, FOLD_GROUP))
                row_out(("k", 0, FOLD_GROUP), nc.scalar.copy)
            if chunk == 0 and at == FIRST_ROWS[1]:
                row(("q", 0, 1))
                row_out(("q", 0, 1), engine_copy(FIRST_ROW_BY))
            if chunk == 0 and at == FILL_AT:
                for tg in TRANSPOSED[1]:
                    make_biases(GROUPS + tg)
                fill_terms()

        def gpsimd_work(chunk, g):
            b, c = divmod(chunk, CHUNKS)
            work = []
            if g == 1 and chunk < BATCH * CHUNKS - 2 and is_in_fold(queries_of(chunk + 2)):
                work.append((split, queries_of(chunk + 2)))
            if g == 3 and chunk == 0:
                work.append((group_values, 1))
            if g == 1 and chunk == 1:
                work.append((split, ("k", 1, FOLD_GROUP)))
            if 0 < chunk < BATCH * CHUNKS - 1:
                ahead_groups = TRANSPOSED[chunk + 1]
                for k, tg in enumerate(ahead_groups):
                    if g == (1 if k == 0 else 3):
                        work.append((make_biases, (chunk + 1) * GROUPS + tg))
            if work and chunk:
                scales = packed[unit_of_last_quantise[0]][1]
                nc.gpsimd.tensor_copy(out=seen[:], in_=scales[:, unit_of_last_quantise[1], 0:PACK])
            for task, argument in work:
                task(argument)

        def spread_mask():
            turned = score_psum.tile([P, PACK, P], BF16, tag="scores", name="turned_mask")
            for t in range(PACK):
                nc.tensor.transpose(turned[:, t, :], mask_sb[:, t:GROUP:PACK], identity[:])
            nc.vector.tensor_scalar(
                out=mask_term[:].rearrange("p b g t -> p (b g) t"),
                in0=turned[:, :, 0 : BATCH * GROUPS].rearrange("p t g -> p g t"),
                scalar1=-MASK_BIAS,
                scalar2=MASK_BIAS,
                op0=ALU.mult,
                op1=ALU.add,
            )

        squares_by_scalar(q0)
        flip(q0)
        flip(k0)
        row(q0)
        flip_out(q0, nc.vector.tensor_copy)
        squares_by_scalar(k0)
        flip_out(k0, nc.vector.tensor_copy)
        row_out(q0, nc.vector.tensor_copy)
        spread_mask()
        add_mask(k0)
        squares_by_scalar(k1)
        flip(k1)
        flip_out(k1, nc.vector.tensor_copy)
        group_values(0)

        for u in range(UNITS):
            b, c, g = unit_indices(u)
            last = u == UNITS - 1
            for t in range(PACK):
                if t == FOLD_SLOT and is_folded_by_parts(b, c, FOLD_GROUP):
                    folded_tile_by_parts(u - g + FOLD_GROUP, g)
                chunk = u // GROUPS
                tiles = [(tg, a) for tg in TRANSPOSED[chunk] for a in range(Q_TILES)]
                if chunk == BATCH * CHUNKS - 1 and len(tiles) == 4:
                    slots = LAST_FOLD_SLOTS
                else:
                    slots = FOLD_SLOTS if len(tiles) == 4 else FOLD_SLOTS2
                if tiles and (g, t) in slots:
                    tg, a = tiles[slots.index((g, t))]
                    folded_tile_by_transposes(u - g + tg, a)
                if u == LAST_SUBTRACTED:
                    for t2 in (2 * t % PACK, 2 * t % PACK + 1):
                        scores_to_logits(u, t2, t // 2 * (CHUNK // 2), (t // 2 + 1) * (CHUNK // 2))
                elif not is_folded(b, c, g):
                    scores_to_logits(u, t, 0, CHUNK)
                ahead(u // GROUPS, g, t)
                if u == 0 and t == 1:
                    squares_by_scalar(k2)
                    squares_by_scalar(k3)
                    squares_by_scalar(q1)
                    flip(k2)
                    flip_out(k2, nc.vector.tensor_copy)
                    add_mask(k1)
                if u == 0 and t == 3:
                    flip(k3)
                    flip_out(k3, nc.vector.tensor_copy)
                    add_mask(k2)
                    add_mask(k3)
            if u == VALUES_AT:
                quantise_values(0)
            if u == 2 * GROUPS:
                quantise_values(1)
            if u % 2 == 1 and u > 1:
                if u > 3:
                    quantise_pair(u - 2)
                gpsimd_work(b * CHUNKS + c, g)
            if u == FIRST_QUANT:
                quantise_pair(1)
            done = u // GROUPS - 1
            if done >= 0 and g == 2:
                sums[done] = out_psum.tile([P, Q_TILES, DIM], F32, name="acc")
                for a in range(Q_TILES):
                    attn_times_values(done // CHUNKS, done % CHUNKS, a, sums[done][:, a, :])
            if done >= 0 and g == 3:
                result = result_pool.tile([P, Q_TILES, DIM], F32)
                engine_copy(RESULT_BY[done])(out=result[:], in_=sums[done][:])
                store(done // CHUNKS, done % CHUNKS, 0, Q_TILES, result[:])
            if u != LAST_SUBTRACTED and not is_folded(b, c, g):
                exponentials(u)

        b, c, g = unit_indices(LAST_SUBTRACTED)
        quantise_part(UNITS - 1, 0, Q_TILES)
        for a in range(Q_TILES):
            exponentials(LAST_SUBTRACTED, a, a + 1)
            quantise_part(LAST_SUBTRACTED, a, a + 1)
        for a in range(Q_TILES):
            acc = score_psum.tile([P, DIM], F32, tag="scores")
            attn_times_values(b, c, a, acc[:])
            result = result_pool.tile([P, DIM], F32, name="last_result")
            nc.vector.tensor_copy(out=result[:], in_=acc[:])
            store(b, c, a, a + 1, result[:].rearrange("p (a d) -> p a d", a=1))
